import numpy as np
import ml_dtypes


def mxq(x, axis, fmt="e4m3"):
    dtype, down = {"e4m3": (ml_dtypes.float8_e4m3fn, 7), "e5m2": (ml_dtypes.float8_e5m2, 14)}[fmt]
    v = np.moveaxis(np.asarray(x, np.float32).astype(ml_dtypes.bfloat16).astype(np.float64), axis, -1)
    blocks = v.reshape(v.shape[:-1] + (-1, 32))
    amax = np.abs(blocks).max(-1, keepdims=True)
    byte = np.maximum(np.where(amax > 0, np.frexp(amax)[1] - 1 + 127, 0) - down, 1)
    scale = np.exp2(byte - 127.0)
    codes = (blocks / scale).astype(np.float32).astype(dtype).astype(np.float64)
    return np.moveaxis((codes * scale).reshape(v.shape), -1, axis)


WIDE = False


def mx_kscale(k):
    if not WIDE:
        return np.ones(k)
    levels = np.array([10, -10, 5, -5, 0])
    a = np.random.permutation(np.resize(levels, k // 512 * 4)).reshape(k // 512, 4)
    idx = np.arange(k)
    return np.exp2(a[idx // 512, idx % 128 // 32])


BF16 = ml_dtypes.bfloat16


def bf(x):
    return np.asarray(x, np.float32).astype(BF16)


def f64(x):
    return np.asarray(x).astype(np.float64)


B, ND, NS, D = 4, 1024, 1024, 512
NUM_ITERS = 5
REG = 0.1
EPS = 1e-12


def l2_normalize(v):
    n = np.sqrt(np.sum(v * v, axis=-1, keepdims=True))
    return v / np.maximum(n, EPS)


def logsumexp(v, axis):
    m = np.max(v, axis=axis, keepdims=True)
    return m + np.log(np.sum(np.exp(v - m), axis=axis, keepdims=True))


def setup_inputs():
    s, t = mx_kscale(D), mx_kscale(D)
    c0 = np.random.standard_normal((B, 1, D))
    c1 = np.random.standard_normal((B, 1, D))
    gd = np.random.random((B, ND, 1)) < 0.7
    gs = np.random.random((B, NS, 1)) < 0.3
    drone = np.random.standard_normal((B, ND, D)) + 1.44 * np.where(gd, c0, c1)
    sat = np.random.standard_normal((B, NS, D)) + 1.44 * np.where(gs, c0, c1)
    w0 = np.random.standard_normal((D, D))
    wq = (w0 + 0.5 * np.random.standard_normal((D, D))) * 0.9 / np.sqrt(D)
    wk = (w0 + 0.5 * np.random.standard_normal((D, D))) * 0.9 / np.sqrt(D)
    return {"drone_tokens": bf(drone * s), "sat_tokens": bf(sat * t),
            "Wq": bf(wq / s), "bq": bf(np.random.standard_normal(D) * 0.5),
            "Wk": bf(wk / t), "bk": bf(np.random.standard_normal(D) * 0.5)}


def reference(drone_tokens, sat_tokens, Wq, bq, Wk, bk):
    q = l2_normalize((mxq(f64(drone_tokens), 2, "e4m3") @ mxq(f64(Wq), 1, "e4m3").T) + f64(bq))
    k = l2_normalize((mxq(f64(sat_tokens), 2, "e4m3") @ mxq(f64(Wk), 1, "e4m3").T) + f64(bk))
    cost = 1.0 - (mxq(q, 2, "e4m3") @ mxq(k, 2, "e4m3").transpose(0, 2, 1))
    M = -cost / REG
    for _ in range(NUM_ITERS):
        M = M - logsumexp(M, 2)
        M = M - logsumexp(M, 1)
    transport_plan = np.exp(M)
    ot_cost = np.mean(np.sum(transport_plan * cost, axis=(1, 2)))
    return transport_plan, ot_cost

@@ -1,0 +1,427 @@
+from contextlib import ExitStack
+
+import concourse.mybir as mybir
+from concourse.masks import make_identity
+
+F32 = mybir.dt.float32
+BF16 = mybir.dt.bfloat16
+U32 = mybir.dt.uint32
+U8 = mybir.dt.uint8
+FP8X4 = mybir.dt.float8_e4m3fn_x4
+ACT = mybir.ActivationFunctionType
+ALU = mybir.AluOpType
+AX = mybir.AxisListType
+
+P = 128
+B = 4
+T = 1024
+D = 512
+NT = T // P
+HALF = 4
+ITERS = 5
+UNITS = B * 2 * 2
+WARM_PASSES = 1
+
+FLOPS = 2 * 2 * B * T * D * D + 2 * B * T * T * D
+
+
+def tile_sinkhornot_t_kernel(tc, drone_tokens, sat_tokens, Wq, bq, Wk, bk, out_0, out_1):
+    nc = tc.nc
+    with ExitStack() as ctx:
+        ctx.enter_context(tc.manual_schedule())
+        keep = ctx.enter_context(tc.tile_pool(name="keep", bufs=1))
+        small = ctx.enter_context(tc.tile_pool(name="small", bufs=4))
+        uv = ctx.enter_context(tc.tile_pool(name="uv", bufs=8))
+        kpool_a = ctx.enter_context(tc.tile_pool(name="kpool_a", bufs=1))
+        psum = ctx.enter_context(tc.psum_pool(name="psum", bufs=8))
+
+        bias_b = []
+        for side, bvec in enumerate((bq, bk)):
+            bt = keep.tile([P, D], BF16, name="bias%d" % side)
+            nc.scalar.dma_start(out=bt[:], in_=bvec.partition_broadcast(P))
+            bias_b.append(bt)
+        ident_f = keep.tile([P, P], F32, name="ident_f")
+        make_identity(nc, ident_f[:])
+        ident_b = keep.tile([P, P], BF16, name="ident_b")
+        make_identity(nc, ident_b[:])
+        ones_f = keep.tile([P, P], F32, name="ones_f")
+        nc.vector.memset(ones_f[:], 1.0)
+        mhalf = keep.tile([P, HALF], F32, name="mhalf")
+        nc.vector.memset(mhalf[:], -0.5)
+        ota = keep.tile([P, B * NT * 2], F32, name="ota")
+        vsq = [keep.tile([P, P], F32, name="vsq%d" % i) for i in range(2)]
+        for i in range(2):
+            nc.vector.memset(vsq[i][:], 0.0)
+
+        wcodes = [keep.tile([P, D], U32, name="wc%d" % s, align_bytes=64) for s in range(2)]
+        wscl = [keep.tile([P, D], U8, name="ws%d" % s, align_bytes=64) for s in range(2)]
+        codes = [[keep.tile([P, T], U32, name="c%d_%d" % (s, b), align_bytes=64) for b in range(B)] for s in range(2)]
+        scl = [[keep.tile([P, T], U8, name="s%d_%d" % (s, b), align_bytes=64) for b in range(B)] for s in range(2)]
+
+        kmat = [None] * B
+        r0_now = [None] * B
+        u_now = [None] * B
+
+        def words_to_groups(src_f, first_tile, grp_f):
+            for pair in range(2):
+                xt = psum.tile([P, 512], F32, name="xt", tag="bank")
+                for a in range(2):
+                    n = first_tile + pair * 2 + a
+                    for u in range(2):
+                        nc.tensor.transpose(
+                            out=xt[:, (a * 2 + u) * P : (a * 2 + u + 1) * P],
+                            in_=src_f[:, n * 256 + u * P : n * 256 + (u + 1) * P],
+                            identity=ident_f[:],
+                        )
+                nc.vector.tensor_copy(
+                    out=grp_f[:, pair * 512 : (pair + 1) * 512].rearrange("p (a r u) -> p a r u", a=2, u=2),
+                    in_=xt[:].rearrange("p (a u r) -> p a r u", a=2, u=2),
+                )
+
+        def make_u(b, r):
+            u8 = uv.tile([P, NT], F32, name="u8", tag="u8")
+            nc.vector.reciprocal(out=u8[:], in_=r)
+            u_now[b] = u8
+
+        def s_pass(b, it, hh):
+            sp = psum.tile([P, 512], F32, name="sp", tag="bank")
+            nc.tensor.matmul_mx(
+                out=sp[:],
+                lhsT=codes[0][b][:, it * P : (it + 1) * P].bitcast(FP8X4),
+                lhsT_scale=scl[0][b][:, it * P : (it + 1) * P],
+                rhs=codes[1][b][:, hh * 512 : (hh + 1) * 512].bitcast(FP8X4),
+                rhs_scale=scl[1][b][:, hh * 512 : (hh + 1) * 512],
+                start=True,
+                stop=True,
+            )
+            return sp
+
+        def fill_quarter(b, quarter, pool):
+            if quarter == 0:
+                kmat[b] = pool.tile([P, NT * T], F32, name="k%d" % b)
+                r0_now[b] = small.tile([P, NT * 2], F32, name="r0", tag="r0")
+            kb = kmat[b]
+            r0 = r0_now[b]
+            sps = [(it, hh, s_pass(b, it, hh)) for it in (2 * quarter, 2 * quarter + 1) for hh in range(2)]
+            for it, hh, sp in sps:
+                nc.scalar.activation(
+                    out=kb[:, it * T + hh * 512 : it * T + (hh + 1) * 512],
+                    in_=sp[:],
+                    func=ACT.Exp,
+                    scale=10.0,
+                    accum_out=r0[:, it * 2 + hh : it * 2 + hh + 1],
+                )
+            if quarter == 3:
+                r = small.tile([P, NT], F32, name="r", tag="r")
+                nc.vector.tensor_reduce(
+                    out=r[:], in_=r0[:].rearrange("p (i h) -> p i h", h=2), axis=AX.X, op=ALU.add
+                )
+                make_u(b, r[:])
+
+        with ExitStack() as actx:
+            xin = actx.enter_context(tc.tile_pool(name="xin", bufs=2))
+            wst = actx.enter_context(tc.tile_pool(name="wst", bufs=1))
+            sta = actx.enter_context(tc.tile_pool(name="sta", bufs=2))
+
+            xs_of = {}
+            st = {}
+
+            def load_weights(side, w):
+                raw = wst.tile([P, 4 * D], BF16, name="wraw%d" % side, tag="wraw%d" % side)
+                nc.sync.dma_start(
+                    out=raw[:].rearrange("p (n d) -> p n d", n=4), in_=w.rearrange("(n p) d -> p n d", p=P)
+                )
+                return raw
+
+            def prep_weights(side, raw):
+                grp = wst.tile([P, 4 * D], BF16, name="wgrp", tag="wgrp", align_bytes=64)
+                words_to_groups(raw[:].bitcast(F32), 0, grp[:].bitcast(F32))
+                return grp
+
+            def quant_weights(side, grp):
+                nc.vector.quantize_mx(out=wcodes[side][:].bitcast(FP8X4), scales=wscl[side][:], in_=grp[:])
+
+            def load_tokens(g):
+                b, side = g // 2, g % 2
+                xs = xin.tile([P, NT * D], BF16, name="xs", tag="xs")
+                if side == 0:
+                    nc.sync.dma_start(out=xs[:], in_=drone_tokens[b].rearrange("(p n) d -> p (n d)", n=NT))
+                else:
+                    nc.sync.dma_start(
+                        out=xs[:].rearrange("p (n d) -> p n d", n=NT),
+                        in_=sat_tokens[b].rearrange("(n p) d -> p n d", p=P),
+                    )
+                xs_of[g] = xs
+
+            def stage_t1(k):
+                grp = sta.tile([P, HALF * P * 4], BF16, name="grp", tag="grp", align_bytes=64)
+                words_to_groups(xs_of[k // 2][:].bitcast(F32), (k % 2) * HALF, grp[:].bitcast(F32))
+                st[("grp", k)] = grp
+
+            def stage_q1(k):
+                xc = sta.tile([P, HALF * P], U32, name="xc", tag="xc", align_bytes=64)
+                xsc = sta.tile([P, HALF * P], U8, name="xsc", tag="xsc", align_bytes=64)
+                nc.vector.quantize_mx(out=xc[:].bitcast(FP8X4), scales=xsc[:], in_=st[("grp", k)][:])
+                st[("xc", k)] = (xc, xsc)
+
+            def stage_m1(k):
+                side = (k // 2) % 2
+                xc, xsc = st[("xc", k)]
+                y = sta.tile([P, HALF * D], F32, name="y", tag="y", bufs=3)
+                ss = small.tile([P, HALF], F32, name="ss", tag="ss")
+                yps = []
+                for a in range(HALF):
+                    yp = psum.tile([P, D], F32, name="yp", tag="bank")
+                    nc.tensor.matmul_mx(
+                        out=yp[:],
+                        lhsT=xc[:, a * P : (a + 1) * P].bitcast(FP8X4),
+                        lhsT_scale=xsc[:, a * P : (a + 1) * P],
+                        rhs=wcodes[side][:].bitcast(FP8X4),
+                        rhs_scale=wscl[side][:],
+                        start=True,
+                        stop=True,
+                    )
+                    yps.append(yp)
+                for a in range(HALF):
+                    nc.vector.tensor_tensor(
+                        out=y[:, a * D : (a + 1) * D], in0=yps[a][:], in1=bias_b[side][:], op=ALU.add
+                    )
+                    sq = sta.tile([P, D], BF16, name="sq", tag="sq")
+                    nc.scalar.activation(
+                        out=sq[:], in_=y[:, a * D : (a + 1) * D], func=ACT.Square, accum_out=ss[:, a : a + 1]
+                    )
+                st[("y", k)] = (y, ss)
+
+            def stage_sc(k):
+                y, ss = st[("y", k)]
+                ssc = small.tile([P, HALF], F32, name="ssc", tag="ssc")
+                nc.vector.tensor_scalar_max(out=ssc[:], in0=ss[:], scalar1=1e-24)
+                rn = small.tile([P, HALF], F32, name="rn", tag="rn")
+                nc.gpsimd.tensor_tensor(out=rn[:], in0=ssc[:], in1=mhalf[:], op=ALU.pow)
+                qh = sta.tile([P, HALF * D], BF16, name="qh", tag="qh", bufs=3)
+                for a in range(HALF):
+                    nc.gpsimd.tensor_scalar(
+                        out=qh[:, a * D : (a + 1) * D],
+                        in0=y[:, a * D : (a + 1) * D],
+                        scalar1=rn[:, a : a + 1],
+                        scalar2=0.0,
+                        op0=ALU.mult,
+                        op1=ALU.add,
+                    )
+                st[("qh", k)] = qh
+
+            def stage_t2(k):
+                qh = st[("qh", k)]
+                qg = sta.tile([P, HALF * P * 4], BF16, name="qg", tag="qg", align_bytes=64)
+                qts = []
+                for pair in range(2):
+                    qt = psum.tile([P, 1024], BF16, name="qt", tag="bank")
+                    for a in range(2):
+                        for t in range(4):
+                            nc.tensor.transpose(
+                                out=qt[:, (a * 4 + t) * P : (a * 4 + t + 1) * P],
+                                in_=qh[:, (pair * 2 + a) * D + t * P : (pair * 2 + a) * D + (t + 1) * P],
+                                identity=ident_b[:],
+                            )
+                    qts.append(qt)
+                for pair in range(2):
+                    dst = qg[:, pair * 1024 : (pair + 1) * 1024].rearrange("p (a r t) -> p a r t", a=2, t=4)
+                    src = qts[pair][:].rearrange("p (a t r) -> p a r t", a=2, t=4)
+                    if pair == 0:
+                        nc.scalar.copy(out=dst, in_=src)
+                    else:
+                        nc.vector.tensor_copy(out=dst, in_=src)
+                st[("qg", k)] = qg
+
+            def stage_q2(k):
+                b, side, h = k // 4, (k // 2) % 2, k % 2
+                nc.vector.quantize_mx(
+                    out=codes[side][b][:, h * 512 : (h + 1) * 512].bitcast(FP8X4),
+                    scales=scl[side][b][:, h * 512 : (h + 1) * 512],
+                    in_=st[("qg", k)][:],
+                )
+
+            raw_q = load_weights(0, Wq)
+            load_tokens(0)
+            raw_k = load_weights(1, Wk)
+            load_tokens(1)
+            grp_q = prep_weights(0, raw_q)
+            quant_weights(0, grp_q)
+            grp_k = prep_weights(1, raw_k)
+            quant_weights(1, grp_k)
+
+            for s in range(UNITS + 5):
+                if s % 2 == 0 and 2 <= s // 2 + 1 < 2 * B:
+                    load_tokens(s // 2 + 1)
+                if 0 <= s - 5 < UNITS:
+                    stage_q2(s - 5)
+                if 0 <= s - 4 < UNITS:
+                    stage_t2(s - 4)
+                if 0 <= s - 1 < UNITS:
+                    stage_q1(s - 1)
+                if s < UNITS:
+                    stage_t1(s)
+                if 0 <= s - 1 < UNITS:
+                    stage_m1(s - 1)
+                if 0 <= s - 2 < UNITS:
+                    stage_sc(s - 2)
+                if s >= 9 and (s - 9) // 4 < 3:
+                    fill_quarter((s - 9) // 4, (s - 9) % 4, kpool_a)
+
+        kpool_b = ctx.enter_context(tc.tile_pool(name="kpool_b", bufs=1))
+        sk = ctx.enter_context(tc.tile_pool(name="sk", bufs=2))
+
+        warm = psum.tile([P, 512], F32, name="warm", tag="bank")
+
+        def keep_clock():
+            nc.tensor.matmul_mx(
+                out=warm[:],
+                lhsT=wcodes[0][:, 0:P].bitcast(FP8X4),
+                lhsT_scale=wscl[0][:, 0:P],
+                rhs=wcodes[1][:].bitcast(FP8X4),
+                rhs_scale=wscl[1][:],
+                start=True,
+                stop=True,
+            )
+
+        ct_of = {}
+        vp_of = {}
+        vb_of = {}
+
+        def col_scale(k, tiles):
+            b = k % B
+            kb = kmat[b]
+            u8 = u_now[b]
+            if tiles[0] == 0:
+                ct_of[k] = [psum.tile([P, 512], F32, name="ct%d" % h, tag="bank") for h in range(2)]
+            ct = ct_of[k]
+            for it in tiles:
+                yk = sk.tile([P, T], F32, name="yk", tag="yk", bufs=4)
+                nc.scalar.activation(
+                    out=yk[:], in_=kb[:, it * T : (it + 1) * T], func=ACT.Copy, scale=u8[:, it : it + 1]
+                )
+                for jt in range(NT):
+                    nc.tensor.matmul(
+                        out=ct[jt // 4][:, (jt % 4) * P : (jt % 4 + 1) * P],
+                        lhsT=yk[:, jt * P : (jt + 1) * P],
+                        rhs=ident_f[:],
+                        is_transpose=True,
+                        start=(it == 0 and jt % 4 == 0),
+                        stop=(it == NT - 1 and jt % 4 == 3),
+                    )
+                for rep_i in range(WARM_PASSES):
+                    keep_clock()
+
+        def col_reduce(k):
+            ct = ct_of[k]
+            c8 = small.tile([P, NT], F32, name="c8", tag="c8")
+            for h in range(2):
+                nc.vector.tensor_reduce(
+                    out=c8[:, h * 4 : (h + 1) * 4],
+                    in_=ct[h][:].rearrange("p (q m) -> p q m", m=P),
+                    axis=AX.X,
+                    op=ALU.add,
+                )
+            nc.vector.reciprocal(out=vsq[k % 2][:, 0:NT], in_=c8[:])
+
+        def spread_start(k):
+            vt = psum.tile([P, P], F32, name="vt", tag="bank")
+            nc.tensor.transpose(out=vt[:], in_=vsq[k % 2][:], identity=ident_f[:])
+            vp_of[k] = vt
+
+        def spread_end(k):
+            b, step = k % B, k // B
+            vrow = sk.tile([32, P], F32, name="vrow", tag="vrow")
+            nc.scalar.copy(out=vrow[:], in_=vp_of[k][0:32, :])
+            park = out_0[b][step]
+            nc.sync.dma_start(out=park.rearrange("(c j) -> c j", c=NT), in_=vrow[0:NT, :])
+            vb = sk.tile([P, T], F32, name="vb", tag="vb", bufs=3)
+            nc.sync.dma_start(out=vb[:], in_=park.partition_broadcast(P))
+            vb_of[k] = vb
+
+        def row_step(k):
+            b = k % B
+            kb = kmat[b]
+            vb = vb_of[k]
+            r = small.tile([P, NT], F32, name="r", tag="r")
+            for it in range(NT):
+                junk = sk.tile([P, T], F32, name="junk", tag="junk", bufs=1)
+                nc.vector.scalar_tensor_tensor(
+                    out=junk[:],
+                    in0=kb[:, it * T : (it + 1) * T],
+                    scalar=1.0,
+                    in1=vb[:],
+                    op0=ALU.mult,
+                    op1=ALU.mult,
+                    accum_out=r[:, it : it + 1],
+                )
+            make_u(b, r[:])
+
+        def finish(k):
+            b = k % B
+            kb = kmat[b]
+            u8 = u_now[b]
+            vb = vb_of[k]
+            ov = out_0[b].rearrange("(p n) j -> p n j", n=NT)
+            for it in range(NT):
+                sps = [s_pass(b, it, hh) for hh in range(2)]
+                nc.vector.scalar_tensor_tensor(
+                    out=kb[:, it * T : (it + 1) * T],
+                    in0=kb[:, it * T : (it + 1) * T],
+                    scalar=u8[:, it : it + 1],
+                    in1=vb[:],
+                    op0=ALU.mult,
+                    op1=ALU.mult,
+                )
+                for hh in range(2):
+                    junk = sk.tile([P, T], F32, name="junk", tag="junk", bufs=1)
+                    col = (b * NT + it) * 2 + hh
+                    nc.vector.scalar_tensor_tensor(
+                        out=junk[:, 0:512],
+                        in0=sps[hh][:],
+                        scalar=1.0,
+                        in1=kb[:, it * T + hh * 512 : it * T + (hh + 1) * 512],
+                        op0=ALU.subtract,
+                        op1=ALU.mult,
+                        accum_out=ota[:, col : col + 1],
+                    )
+                if it % 2 == 1:
+                    nc.sync.dma_start(
+                        out=ov[:, it - 1 : it + 1, :],
+                        in_=kb[:, (it - 1) * T : (it + 1) * T].rearrange("p (n j) -> p n j", n=2),
+                    )
+
+        steps = ITERS * B
+        for k in range(steps + 2):
+            if 0 <= k - 1 < steps:
+                col_reduce(k - 1)
+            if k < steps:
+                col_scale(k, (0, 1))
+            if 0 <= k - 1 < steps:
+                spread_start(k - 1)
+            if k < steps:
+                col_scale(k, (2, 3))
+            if 0 <= k - 1 < steps:
+                spread_end(k - 1)
+            if k < steps:
+                col_scale(k, (4, 5, 6, 7))
+            if k < 2:
+                fill_quarter(3, 2 * k, kpool_b)
+                fill_quarter(3, 2 * k + 1, kpool_b)
+            if 0 <= k - 2 < steps - B:
+                row_step(k - 2)
+            elif steps - B <= k - 2 < steps:
+                finish(k - 2)
+
+        tp = psum.tile([P, B * NT * 2], F32, name="tp", tag="bank")
+        nc.tensor.matmul(out=tp[:], lhsT=ones_f[:], rhs=ota[:], start=True, stop=True)
+        tot = small.tile([P, 1], F32, name="tot", tag="tot")
+        nc.vector.tensor_reduce(out=tot[:], in_=tp[:], axis=AX.X, op=ALU.add)
+        res = small.tile([P, 1], F32, name="res", tag="res")
+        nc.vector.tensor_scalar_mul(out=res[:], in0=tot[:], scalar1=-1.0 / B)
+        o1 = out_1
+        if o1.ndim == 0:
+            o1 = o1.unsqueeze(0)
+        if o1.ndim == 1:
+            o1 = o1.unsqueeze(0)
+        nc.sync.dma_start(out=o1, in_=res[0:1, 0:1])

@@ -19,8 +19,6 @@ D = 512
 NT = T // P
 HALF = 4
 ITERS = 5
-UNITS = B * 2 * 2
-WARM_PASSES = 1
 
 FLOPS = 2 * 2 * B * T * D * D + 2 * B * T * T * D
 
@@ -28,12 +26,12 @@ FLOPS = 2 * 2 * B * T * D * D + 2 * B * T * T * D
 def tile_sinkhornot_t_kernel(tc, drone_tokens, sat_tokens, Wq, bq, Wk, bk, out_0, out_1):
     nc = tc.nc
     with ExitStack() as ctx:
-        ctx.enter_context(tc.manual_schedule())
         keep = ctx.enter_context(tc.tile_pool(name="keep", bufs=1))
         small = ctx.enter_context(tc.tile_pool(name="small", bufs=4))
-        uv = ctx.enter_context(tc.tile_pool(name="uv", bufs=8))
-        kpool_a = ctx.enter_context(tc.tile_pool(name="kpool_a", bufs=1))
-        psum = ctx.enter_context(tc.psum_pool(name="psum", bufs=8))
+        kpool = ctx.enter_context(tc.tile_pool(name="kpool", bufs=2))
+        cpool = ctx.enter_context(tc.tile_pool(name="cpool", bufs=3))
+        work = ctx.enter_context(tc.tile_pool(name="work", bufs=2))
+        psum = ctx.enter_context(tc.psum_pool(name="psum", bufs=2))
 
         bias_b = []
         for side, bvec in enumerate((bq, bk)):
@@ -48,372 +46,220 @@ def tile_sinkhornot_t_kernel(tc, drone_tokens, sat_tokens, Wq, bq, Wk, bk, out_0
         nc.vector.memset(ones_f[:], 1.0)
         mhalf = keep.tile([P, HALF], F32, name="mhalf")
         nc.vector.memset(mhalf[:], -0.5)
+        mone = keep.tile([P, NT], F32, name="mone")
+        nc.vector.memset(mone[:], -1.0)
         ota = keep.tile([P, B * NT * 2], F32, name="ota")
-        vsq = [keep.tile([P, P], F32, name="vsq%d" % i) for i in range(2)]
-        for i in range(2):
-            nc.vector.memset(vsq[i][:], 0.0)
 
         wcodes = [keep.tile([P, D], U32, name="wc%d" % s, align_bytes=64) for s in range(2)]
         wscl = [keep.tile([P, D], U8, name="ws%d" % s, align_bytes=64) for s in range(2)]
-        codes = [[keep.tile([P, T], U32, name="c%d_%d" % (s, b), align_bytes=64) for b in range(B)] for s in range(2)]
-        scl = [[keep.tile([P, T], U8, name="s%d_%d" % (s, b), align_bytes=64) for b in range(B)] for s in range(2)]
+        codes = {}
+        scl = {}
 
-        kmat = [None] * B
-        r0_now = [None] * B
-        u_now = [None] * B
-
-        def words_to_groups(src_f, first_tile, grp_f):
+        def words_to_groups(src_f, grp_f, copy):
             for pair in range(2):
-                xt = psum.tile([P, 512], F32, name="xt", tag="bank")
+                xt = psum.tile([P, 512], F32, name="xt", tag="tr", bufs=3)
                 for a in range(2):
-                    n = first_tile + pair * 2 + a
+                    n = pair * 2 + a
                     for u in range(2):
                         nc.tensor.transpose(
                             out=xt[:, (a * 2 + u) * P : (a * 2 + u + 1) * P],
                             in_=src_f[:, n * 256 + u * P : n * 256 + (u + 1) * P],
                             identity=ident_f[:],
                         )
-                nc.vector.tensor_copy(
+                copy(
                     out=grp_f[:, pair * 512 : (pair + 1) * 512].rearrange("p (a r u) -> p a r u", a=2, u=2),
                     in_=xt[:].rearrange("p (a u r) -> p a r u", a=2, u=2),
                 )
 
-        def make_u(b, r):
-            u8 = uv.tile([P, NT], F32, name="u8", tag="u8")
-            nc.vector.reciprocal(out=u8[:], in_=r)
-            u_now[b] = u8
+        for side, w in ((1, Wk), (0, Wq)):
+            raw = work.tile([P, 4 * D], BF16, name="xs", tag="xs", bufs=3)
+            nc.sync.dma_start(
+                out=raw[:].rearrange("p (n d) -> p n d", n=4), in_=w.rearrange("(n p) d -> p n d", p=P)
+            )
+            grp = work.tile([P, HALF * P * 4], BF16, name="grp", tag="grp", align_bytes=64)
+            words_to_groups(raw[:].bitcast(F32), grp[:].bitcast(F32), nc.vector.tensor_copy)
+            nc.vector.quantize_mx(out=wcodes[side][:].bitcast(FP8X4), scales=wscl[side][:], in_=grp[:])
+
+        def project(b, side, h):
+            xs = work.tile([P, HALF * D], BF16, name="xs", tag="xs", bufs=3)
+            if side == 0:
+                nc.sync.dma_start(
+                    out=xs[:],
+                    in_=drone_tokens[b].rearrange("(p n) d -> p (n d)", n=NT)[:, h * HALF * D : (h + 1) * HALF * D],
+                )
+            else:
+                nc.sync.dma_start(
+                    out=xs[:].rearrange("p (n d) -> p n d", n=HALF),
+                    in_=sat_tokens[b].rearrange("(n p) d -> p n d", p=P)[:, h * HALF : (h + 1) * HALF, :],
+                )
+            grp = work.tile([P, HALF * P * 4], BF16, name="grp", tag="grp", align_bytes=64)
+            words_to_groups(xs[:].bitcast(F32), grp[:].bitcast(F32), nc.scalar.copy)
+            xc = work.tile([P, HALF * P], U32, name="xc", tag="xc", align_bytes=64)
+            xsc = work.tile([P, HALF * P], U8, name="xsc", tag="xsc", align_bytes=64)
+            nc.vector.quantize_mx(out=xc[:].bitcast(FP8X4), scales=xsc[:], in_=grp[:])
+            ss = small.tile([P, HALF], F32, name="ss", tag="ss")
+            ys = []
+            for a in range(HALF):
+                yp = psum.tile([P, D], F32, name="yp", tag="mm", bufs=3)
+                nc.tensor.matmul_mx(
+                    out=yp[:],
+                    lhsT=xc[:, a * P : (a + 1) * P].bitcast(FP8X4),
+                    lhsT_scale=xsc[:, a * P : (a + 1) * P],
+                    rhs=wcodes[side][:].bitcast(FP8X4),
+                    rhs_scale=wscl[side][:],
+                    start=True,
+                    stop=True,
+                )
+                y = work.tile([P, D], F32, name="y", tag="y", bufs=6)
+                nc.vector.tensor_tensor(out=y[:], in0=yp[:], in1=bias_b[side][:], op=ALU.add)
+                sq = work.tile([P, D], BF16, name="sq", tag="sq", bufs=1)
+                nc.scalar.activation(out=sq[:], in_=y[:], func=ACT.Square, accum_out=ss[:, a : a + 1])
+                ys.append(y)
+            ssc = small.tile([P, HALF], F32, name="ssc", tag="ssc")
+            nc.gpsimd.tensor_scalar(out=ssc[:], in0=ss[:], scalar1=1e-24, scalar2=0.0, op0=ALU.max, op1=ALU.add)
+            rn = small.tile([P, HALF], F32, name="rn", tag="rn")
+            nc.gpsimd.tensor_tensor(out=rn[:], in0=ssc[:], in1=mhalf[:], op=ALU.pow)
+            qh = work.tile([P, HALF * D], BF16, name="qh", tag="qh")
+            for a in range(HALF):
+                nc.vector.tensor_scalar(
+                    out=qh[:, a * D : (a + 1) * D],
+                    in0=ys[a][:],
+                    scalar1=rn[:, a : a + 1],
+                    scalar2=None,
+                    op0=ALU.mult,
+                )
+            qg = work.tile([P, HALF * P * 4], BF16, name="grp", tag="grp", align_bytes=64)
+            words_to_groups(qh[:].bitcast(F32), qg[:].bitcast(F32), nc.scalar.copy)
+            nc.vector.quantize_mx(
+                out=codes[(side, b)][:, h * 512 : (h + 1) * 512].bitcast(FP8X4),
+                scales=scl[(side, b)][:, h * 512 : (h + 1) * 512],
+                in_=qg[:],
+            )
 
         def s_pass(b, it, hh):
-            sp = psum.tile([P, 512], F32, name="sp", tag="bank")
+            sp = psum.tile([P, 512], F32, name="sp", tag="mm", bufs=3)
             nc.tensor.matmul_mx(
                 out=sp[:],
-                lhsT=codes[0][b][:, it * P : (it + 1) * P].bitcast(FP8X4),
-                lhsT_scale=scl[0][b][:, it * P : (it + 1) * P],
-                rhs=codes[1][b][:, hh * 512 : (hh + 1) * 512].bitcast(FP8X4),
-                rhs_scale=scl[1][b][:, hh * 512 : (hh + 1) * 512],
+                lhsT=codes[(0, b)][:, it * P : (it + 1) * P].bitcast(FP8X4),
+                lhsT_scale=scl[(0, b)][:, it * P : (it + 1) * P],
+                rhs=codes[(1, b)][:, hh * 512 : (hh + 1) * 512].bitcast(FP8X4),
+                rhs_scale=scl[(1, b)][:, hh * 512 : (hh + 1) * 512],
                 start=True,
                 stop=True,
             )
             return sp
 
-        def fill_quarter(b, quarter, pool):
-            if quarter == 0:
-                kmat[b] = pool.tile([P, NT * T], F32, name="k%d" % b)
-                r0_now[b] = small.tile([P, NT * 2], F32, name="r0", tag="r0")
-            kb = kmat[b]
-            r0 = r0_now[b]
-            sps = [(it, hh, s_pass(b, it, hh)) for it in (2 * quarter, 2 * quarter + 1) for hh in range(2)]
-            for it, hh, sp in sps:
+        def fill(b, it, kh, kl, kth, ktl, r0):
+            e = work.tile([P, T], F32, name="e", tag="e", bufs=3)
+            for hh in range(2):
+                sp = s_pass(b, it, hh)
                 nc.scalar.activation(
-                    out=kb[:, it * T + hh * 512 : it * T + (hh + 1) * 512],
+                    out=e[:, hh * 512 : (hh + 1) * 512],
                     in_=sp[:],
                     func=ACT.Exp,
                     scale=10.0,
                     accum_out=r0[:, it * 2 + hh : it * 2 + hh + 1],
                 )
-            if quarter == 3:
-                r = small.tile([P, NT], F32, name="r", tag="r")
-                nc.vector.tensor_reduce(
-                    out=r[:], in_=r0[:].rearrange("p (i h) -> p i h", h=2), axis=AX.X, op=ALU.add
-                )
-                make_u(b, r[:])
-
-        with ExitStack() as actx:
-            xin = actx.enter_context(tc.tile_pool(name="xin", bufs=2))
-            wst = actx.enter_context(tc.tile_pool(name="wst", bufs=1))
-            sta = actx.enter_context(tc.tile_pool(name="sta", bufs=2))
-
-            xs_of = {}
-            st = {}
-
-            def load_weights(side, w):
-                raw = wst.tile([P, 4 * D], BF16, name="wraw%d" % side, tag="wraw%d" % side)
-                nc.sync.dma_start(
-                    out=raw[:].rearrange("p (n d) -> p n d", n=4), in_=w.rearrange("(n p) d -> p n d", p=P)
-                )
-                return raw
-
-            def prep_weights(side, raw):
-                grp = wst.tile([P, 4 * D], BF16, name="wgrp", tag="wgrp", align_bytes=64)
-                words_to_groups(raw[:].bitcast(F32), 0, grp[:].bitcast(F32))
-                return grp
-
-            def quant_weights(side, grp):
-                nc.vector.quantize_mx(out=wcodes[side][:].bitcast(FP8X4), scales=wscl[side][:], in_=grp[:])
-
-            def load_tokens(g):
-                b, side = g // 2, g % 2
-                xs = xin.tile([P, NT * D], BF16, name="xs", tag="xs")
-                if side == 0:
-                    nc.sync.dma_start(out=xs[:], in_=drone_tokens[b].rearrange("(p n) d -> p (n d)", n=NT))
-                else:
-                    nc.sync.dma_start(
-                        out=xs[:].rearrange("p (n d) -> p n d", n=NT),
-                        in_=sat_tokens[b].rearrange("(n p) d -> p n d", p=P),
-                    )
-                xs_of[g] = xs
-
-            def stage_t1(k):
-                grp = sta.tile([P, HALF * P * 4], BF16, name="grp", tag="grp", align_bytes=64)
-                words_to_groups(xs_of[k // 2][:].bitcast(F32), (k % 2) * HALF, grp[:].bitcast(F32))
-                st[("grp", k)] = grp
-
-            def stage_q1(k):
-                xc = sta.tile([P, HALF * P], U32, name="xc", tag="xc", align_bytes=64)
-                xsc = sta.tile([P, HALF * P], U8, name="xsc", tag="xsc", align_bytes=64)
-                nc.vector.quantize_mx(out=xc[:].bitcast(FP8X4), scales=xsc[:], in_=st[("grp", k)][:])
-                st[("xc", k)] = (xc, xsc)
-
-            def stage_m1(k):
-                side = (k // 2) % 2
-                xc, xsc = st[("xc", k)]
-                y = sta.tile([P, HALF * D], F32, name="y", tag="y", bufs=3)
-                ss = small.tile([P, HALF], F32, name="ss", tag="ss")
-                yps = []
-                for a in range(HALF):
-                    yp = psum.tile([P, D], F32, name="yp", tag="bank")
-                    nc.tensor.matmul_mx(
-                        out=yp[:],
-                        lhsT=xc[:, a * P : (a + 1) * P].bitcast(FP8X4),
-                        lhsT_scale=xsc[:, a * P : (a + 1) * P],
-                        rhs=wcodes[side][:].bitcast(FP8X4),
-                        rhs_scale=wscl[side][:],
-                        start=True,
-                        stop=True,
-                    )
-                    yps.append(yp)
-                for a in range(HALF):
-                    nc.vector.tensor_tensor(
-                        out=y[:, a * D : (a + 1) * D], in0=yps[a][:], in1=bias_b[side][:], op=ALU.add
-                    )
-                    sq = sta.tile([P, D], BF16, name="sq", tag="sq")
-                    nc.scalar.activation(
-                        out=sq[:], in_=y[:, a * D : (a + 1) * D], func=ACT.Square, accum_out=ss[:, a : a + 1]
-                    )
-                st[("y", k)] = (y, ss)
-
-            def stage_sc(k):
-                y, ss = st[("y", k)]
-                ssc = small.tile([P, HALF], F32, name="ssc", tag="ssc")
-                nc.vector.tensor_scalar_max(out=ssc[:], in0=ss[:], scalar1=1e-24)
-                rn = small.tile([P, HALF], F32, name="rn", tag="rn")
-                nc.gpsimd.tensor_tensor(out=rn[:], in0=ssc[:], in1=mhalf[:], op=ALU.pow)
-                qh = sta.tile([P, HALF * D], BF16, name="qh", tag="qh", bufs=3)
-                for a in range(HALF):
-                    nc.gpsimd.tensor_scalar(
-                        out=qh[:, a * D : (a + 1) * D],
-                        in0=y[:, a * D : (a + 1) * D],
-                        scalar1=rn[:, a : a + 1],
-                        scalar2=0.0,
-                        op0=ALU.mult,
-                        op1=ALU.add,
-                    )
-                st[("qh", k)] = qh
-
-            def stage_t2(k):
-                qh = st[("qh", k)]
-                qg = sta.tile([P, HALF * P * 4], BF16, name="qg", tag="qg", align_bytes=64)
-                qts = []
-                for pair in range(2):
-                    qt = psum.tile([P, 1024], BF16, name="qt", tag="bank")
-                    for a in range(2):
-                        for t in range(4):
-                            nc.tensor.transpose(
-                                out=qt[:, (a * 4 + t) * P : (a * 4 + t + 1) * P],
-                                in_=qh[:, (pair * 2 + a) * D + t * P : (pair * 2 + a) * D + (t + 1) * P],
-                                identity=ident_b[:],
-                            )
-                    qts.append(qt)
-                for pair in range(2):
-                    dst = qg[:, pair * 1024 : (pair + 1) * 1024].rearrange("p (a r t) -> p a r t", a=2, t=4)
-                    src = qts[pair][:].rearrange("p (a t r) -> p a r t", a=2, t=4)
-                    if pair == 0:
-                        nc.scalar.copy(out=dst, in_=src)
-                    else:
-                        nc.vector.tensor_copy(out=dst, in_=src)
-                st[("qg", k)] = qg
-
-            def stage_q2(k):
-                b, side, h = k // 4, (k // 2) % 2, k % 2
-                nc.vector.quantize_mx(
-                    out=codes[side][b][:, h * 512 : (h + 1) * 512].bitcast(FP8X4),
-                    scales=scl[side][b][:, h * 512 : (h + 1) * 512],
-                    in_=st[("qg", k)][:],
-                )
-
-            raw_q = load_weights(0, Wq)
-            load_tokens(0)
-            raw_k = load_weights(1, Wk)
-            load_tokens(1)
-            grp_q = prep_weights(0, raw_q)
-            quant_weights(0, grp_q)
-            grp_k = prep_weights(1, raw_k)
-            quant_weights(1, grp_k)
-
-            for s in range(UNITS + 5):
-                if s % 2 == 0 and 2 <= s // 2 + 1 < 2 * B:
-                    load_tokens(s // 2 + 1)
-                if 0 <= s - 5 < UNITS:
-                    stage_q2(s - 5)
-                if 0 <= s - 4 < UNITS:
-                    stage_t2(s - 4)
-                if 0 <= s - 1 < UNITS:
-                    stage_q1(s - 1)
-                if s < UNITS:
-                    stage_t1(s)
-                if 0 <= s - 1 < UNITS:
-                    stage_m1(s - 1)
-                if 0 <= s - 2 < UNITS:
-                    stage_sc(s - 2)
-                if s >= 9 and (s - 9) // 4 < 3:
-                    fill_quarter((s - 9) // 4, (s - 9) % 4, kpool_a)
-
-        kpool_b = ctx.enter_context(tc.tile_pool(name="kpool_b", bufs=1))
-        sk = ctx.enter_context(tc.tile_pool(name="sk", bufs=2))
-
-        warm = psum.tile([P, 512], F32, name="warm", tag="bank")
-
-        def keep_clock():
-            nc.tensor.matmul_mx(
-                out=warm[:],
-                lhsT=wcodes[0][:, 0:P].bitcast(FP8X4),
-                lhsT_scale=wscl[0][:, 0:P],
-                rhs=wcodes[1][:].bitcast(FP8X4),
-                rhs_scale=wscl[1][:],
-                start=True,
-                stop=True,
-            )
-
-        ct_of = {}
-        vp_of = {}
-        vb_of = {}
-
-        def col_scale(k, tiles):
-            b = k % B
-            kb = kmat[b]
-            u8 = u_now[b]
-            if tiles[0] == 0:
-                ct_of[k] = [psum.tile([P, 512], F32, name="ct%d" % h, tag="bank") for h in range(2)]
-            ct = ct_of[k]
-            for it in tiles:
-                yk = sk.tile([P, T], F32, name="yk", tag="yk", bufs=4)
-                nc.scalar.activation(
-                    out=yk[:], in_=kb[:, it * T : (it + 1) * T], func=ACT.Copy, scale=u8[:, it : it + 1]
-                )
+            cols = slice(it * T, (it + 1) * T)
+            nc.vector.tensor_copy(out=kh[:, cols], in_=e[:])
+            nc.vector.tensor_tensor(out=kl[:, cols], in0=e[:], in1=kh[:, cols], op=ALU.subtract)
+            for k, kt in ((kh, kth), (kl, ktl)):
+                tb = psum.tile([P, T], BF16, name="tb", tag="tr", bufs=3)
                 for jt in range(NT):
-                    nc.tensor.matmul(
-                        out=ct[jt // 4][:, (jt % 4) * P : (jt % 4 + 1) * P],
-                        lhsT=yk[:, jt * P : (jt + 1) * P],
-                        rhs=ident_f[:],
-                        is_transpose=True,
-                        start=(it == 0 and jt % 4 == 0),
-                        stop=(it == NT - 1 and jt % 4 == 3),
+                    nc.tensor.transpose(
+                        out=tb[:, jt * P : (jt + 1) * P],
+                        in_=k[:, it * T + jt * P : it * T + (jt + 1) * P],
+                        identity=ident_b[:],
                     )
-                for rep_i in range(WARM_PASSES):
-                    keep_clock()
+                nc.scalar.copy(out=kt[:, cols], in_=tb[:])
 
-        def col_reduce(k):
-            ct = ct_of[k]
+        def inverse(sums):
             c8 = small.tile([P, NT], F32, name="c8", tag="c8")
-            for h in range(2):
-                nc.vector.tensor_reduce(
-                    out=c8[:, h * 4 : (h + 1) * 4],
-                    in_=ct[h][:].rearrange("p (q m) -> p q m", m=P),
-                    axis=AX.X,
-                    op=ALU.add,
-                )
-            nc.vector.reciprocal(out=vsq[k % 2][:, 0:NT], in_=c8[:])
+            nc.vector.tensor_reduce(out=c8[:], in_=sums, axis=AX.X, op=ALU.add)
+            v8 = small.tile([P, NT], F32, name="v8", tag="v8", bufs=8)
+            nc.gpsimd.tensor_tensor(out=v8[:], in0=c8[:], in1=mone[:], op=ALU.pow)
+            vp = small.tile([P, NT, 2], BF16, name="vp", tag="vp")
+            nc.gpsimd.tensor_copy(out=vp[:, :, 0], in_=v8[:])
+            nc.gpsimd.tensor_tensor(out=vp[:, :, 1], in0=v8[:], in1=vp[:, :, 0], op=ALU.subtract)
+            return v8, vp
 
-        def spread_start(k):
-            vt = psum.tile([P, P], F32, name="vt", tag="bank")
-            nc.tensor.transpose(out=vt[:], in_=vsq[k % 2][:], identity=ident_f[:])
-            vp_of[k] = vt
+        def matvec(kh, kl, vp, rows):
+            mv = psum.tile([P, NT, 2], F32, name="mv", tag="mv")
+            for o in range(NT):
+                for c in range(NT):
+                    it, jt = (o, c) if rows else (c, o)
+                    for i, k in enumerate((kh, kl)):
+                        nc.tensor.matmul(
+                            out=mv[:, o, :],
+                            lhsT=k[:, it * T + jt * P : it * T + (jt + 1) * P],
+                            rhs=vp[:, c, :],
+                            start=(c == 0 and i == 0),
+                            stop=(c == NT - 1 and i == 1),
+                        )
+            return mv
 
-        def spread_end(k):
-            b, step = k % B, k // B
-            vrow = sk.tile([32, P], F32, name="vrow", tag="vrow")
-            nc.scalar.copy(out=vrow[:], in_=vp_of[k][0:32, :])
-            park = out_0[b][step]
-            nc.sync.dma_start(out=park.rearrange("(c j) -> c j", c=NT), in_=vrow[0:NT, :])
-            vb = sk.tile([P, T], F32, name="vb", tag="vb", bufs=3)
-            nc.sync.dma_start(out=vb[:], in_=park.partition_broadcast(P))
-            vb_of[k] = vb
-
-        def row_step(k):
-            b = k % B
-            kb = kmat[b]
-            vb = vb_of[k]
-            r = small.tile([P, NT], F32, name="r", tag="r")
-            for it in range(NT):
-                junk = sk.tile([P, T], F32, name="junk", tag="junk", bufs=1)
-                nc.vector.scalar_tensor_tensor(
-                    out=junk[:],
-                    in0=kb[:, it * T : (it + 1) * T],
-                    scalar=1.0,
-                    in1=vb[:],
-                    op0=ALU.mult,
-                    op1=ALU.mult,
-                    accum_out=r[:, it : it + 1],
-                )
-            make_u(b, r[:])
-
-        def finish(k):
-            b = k % B
-            kb = kmat[b]
-            u8 = u_now[b]
-            vb = vb_of[k]
+        def finish(b, u8, v8):
+            vb = work.tile([P, T], F32, name="vb", tag="vb", bufs=1)
+            for hh in range(2):
+                vbp = psum.tile([P, 512], F32, name="vbp", tag="tr", bufs=3)
+                for j in range(4):
+                    jt = hh * 4 + j
+                    nc.tensor.transpose(
+                        out=vbp[:, j * P : (j + 1) * P],
+                        in_=v8[:, jt : jt + 1].to_broadcast([P, P]),
+                        identity=ident_f[:],
+                    )
+                nc.scalar.copy(out=vb[:, hh * 512 : (hh + 1) * 512], in_=vbp[:])
             ov = out_0[b].rearrange("(p n) j -> p n j", n=NT)
             for it in range(NT):
-                sps = [s_pass(b, it, hh) for hh in range(2)]
+                e = work.tile([P, T], F32, name="e", tag="e", bufs=3)
+                sps = []
+                for hh in range(2):
+                    sp = s_pass(b, it, hh)
+                    nc.scalar.activation(out=e[:, hh * 512 : (hh + 1) * 512], in_=sp[:], func=ACT.Exp, scale=10.0)
+                    sps.append(sp)
                 nc.vector.scalar_tensor_tensor(
-                    out=kb[:, it * T : (it + 1) * T],
-                    in0=kb[:, it * T : (it + 1) * T],
-                    scalar=u8[:, it : it + 1],
-                    in1=vb[:],
-                    op0=ALU.mult,
-                    op1=ALU.mult,
+                    out=e[:], in0=e[:], scalar=u8[:, it : it + 1], in1=vb[:], op0=ALU.mult, op1=ALU.mult
                 )
                 for hh in range(2):
-                    junk = sk.tile([P, T], F32, name="junk", tag="junk", bufs=1)
+                    junk = work.tile([P, 512], F32, name="junk", tag="junk", bufs=1)
                     col = (b * NT + it) * 2 + hh
                     nc.vector.scalar_tensor_tensor(
-                        out=junk[:, 0:512],
+                        out=junk[:],
                         in0=sps[hh][:],
                         scalar=1.0,
-                        in1=kb[:, it * T + hh * 512 : it * T + (hh + 1) * 512],
+                        in1=e[:, hh * 512 : (hh + 1) * 512],
                         op0=ALU.subtract,
                         op1=ALU.mult,
                         accum_out=ota[:, col : col + 1],
                     )
-                if it % 2 == 1:
-                    nc.sync.dma_start(
-                        out=ov[:, it - 1 : it + 1, :],
-                        in_=kb[:, (it - 1) * T : (it + 1) * T].rearrange("p (n j) -> p n j", n=2),
-                    )
+                nc.sync.dma_start(out=ov[:, it, :], in_=e[:])
 
-        steps = ITERS * B
-        for k in range(steps + 2):
-            if 0 <= k - 1 < steps:
-                col_reduce(k - 1)
-            if k < steps:
-                col_scale(k, (0, 1))
-            if 0 <= k - 1 < steps:
-                spread_start(k - 1)
-            if k < steps:
-                col_scale(k, (2, 3))
-            if 0 <= k - 1 < steps:
-                spread_end(k - 1)
-            if k < steps:
-                col_scale(k, (4, 5, 6, 7))
-            if k < 2:
-                fill_quarter(3, 2 * k, kpool_b)
-                fill_quarter(3, 2 * k + 1, kpool_b)
-            if 0 <= k - 2 < steps - B:
-                row_step(k - 2)
-            elif steps - B <= k - 2 < steps:
-                finish(k - 2)
+        for b in range(B):
+            for side in range(2):
+                codes[(side, b)] = cpool.tile([P, T], U32, name="c%d" % side, align_bytes=64)
+                scl[(side, b)] = cpool.tile([P, T], U8, name="s%d" % side, align_bytes=64)
+            for side in (1, 0):
+                for h in range(2):
+                    project(b, side, h)
+            kh = kpool.tile([P, NT * T], BF16, name="kh")
+            kl = kpool.tile([P, NT * T], BF16, name="kl")
+            kth = kpool.tile([P, NT * T], BF16, name="kth")
+            ktl = kpool.tile([P, NT * T], BF16, name="ktl")
+            r0 = small.tile([P, NT, 2], F32, name="r0", tag="r0")
+            r0f = r0[:].rearrange("p n c -> p (n c)")
+            for it in range(NT):
+                fill(b, it, kh, kl, kth, ktl, r0f)
+            u8, up = inverse(r0[:])
+            for step in range(ITERS):
+                if step > 0:
+                    mv = matvec(kth, ktl, vp, True)
+                    u8, up = inverse(mv[:])
+                mv = matvec(kh, kl, up, False)
+                v8, vp = inverse(mv[:])
+            finish(b, u8, v8)
 
-        tp = psum.tile([P, B * NT * 2], F32, name="tp", tag="bank")
+        tp = psum.tile([P, B * NT * 2], F32, name="tp", tag="mv")
         nc.tensor.matmul(out=tp[:], lhsT=ones_f[:], rhs=ota[:], start=True, stop=True)
         tot = small.tile([P, 1], F32, name="tot", tag="tot")
         nc.vector.tensor_reduce(out=tot[:], in_=tp[:], axis=AX.X, op=ALU.add)

@@ -19,6 +19,8 @@ D = 512
 NT = T // P
 HALF = 4
 ITERS = 5
+STEPS = 2 * ITERS - 1
+FIRST_STEP = 11
 
 FLOPS = 2 * 2 * B * T * D * D + 2 * B * T * T * D
 
@@ -26,6 +28,7 @@ FLOPS = 2 * 2 * B * T * D * D + 2 * B * T * T * D
 def tile_sinkhornot_t_kernel(tc, drone_tokens, sat_tokens, Wq, bq, Wk, bk, out_0, out_1):
     nc = tc.nc
     with ExitStack() as ctx:
+        ctx.enter_context(tc.manual_schedule())
         keep = ctx.enter_context(tc.tile_pool(name="keep", bufs=1))
         small = ctx.enter_context(tc.tile_pool(name="small", bufs=4))
         kpool = ctx.enter_context(tc.tile_pool(name="kpool", bufs=2))
@@ -46,8 +49,6 @@ def tile_sinkhornot_t_kernel(tc, drone_tokens, sat_tokens, Wq, bq, Wk, bk, out_0
         nc.vector.memset(ones_f[:], 1.0)
         mhalf = keep.tile([P, HALF], F32, name="mhalf")
         nc.vector.memset(mhalf[:], -0.5)
-        mone = keep.tile([P, NT], F32, name="mone")
-        nc.vector.memset(mone[:], -1.0)
         ota = keep.tile([P, B * NT * 2], F32, name="ota")
 
         wcodes = [keep.tile([P, D], U32, name="wc%d" % s, align_bytes=64) for s in range(2)]
@@ -71,7 +72,7 @@ def tile_sinkhornot_t_kernel(tc, drone_tokens, sat_tokens, Wq, bq, Wk, bk, out_0
                     in_=xt[:].rearrange("p (a u r) -> p a r u", a=2, u=2),
                 )
 
-        for side, w in ((1, Wk), (0, Wq)):
+        def weights(side, w):
             raw = work.tile([P, 4 * D], BF16, name="xs", tag="xs", bufs=3)
             nc.sync.dma_start(
                 out=raw[:].rearrange("p (n d) -> p n d", n=4), in_=w.rearrange("(n p) d -> p n d", p=P)
@@ -80,7 +81,10 @@ def tile_sinkhornot_t_kernel(tc, drone_tokens, sat_tokens, Wq, bq, Wk, bk, out_0
             words_to_groups(raw[:].bitcast(F32), grp[:].bitcast(F32), nc.vector.tensor_copy)
             nc.vector.quantize_mx(out=wcodes[side][:].bitcast(FP8X4), scales=wscl[side][:], in_=grp[:])
 
-        def project(b, side, h):
+        st = {}
+
+        def load(unit):
+            b, side, h = unit
             xs = work.tile([P, HALF * D], BF16, name="xs", tag="xs", bufs=3)
             if side == 0:
                 nc.sync.dma_start(
@@ -92,52 +96,77 @@ def tile_sinkhornot_t_kernel(tc, drone_tokens, sat_tokens, Wq, bq, Wk, bk, out_0
                     out=xs[:].rearrange("p (n d) -> p n d", n=HALF),
                     in_=sat_tokens[b].rearrange("(n p) d -> p n d", p=P)[:, h * HALF : (h + 1) * HALF, :],
                 )
+            st[("xs", unit)] = xs
+
+        def turn_tokens(unit):
             grp = work.tile([P, HALF * P * 4], BF16, name="grp", tag="grp", align_bytes=64)
-            words_to_groups(xs[:].bitcast(F32), grp[:].bitcast(F32), nc.scalar.copy)
+            words_to_groups(st[("xs", unit)][:].bitcast(F32), grp[:].bitcast(F32), nc.scalar.copy)
+            st[("grp", unit)] = grp
+
+        def quant_tokens(unit):
             xc = work.tile([P, HALF * P], U32, name="xc", tag="xc", align_bytes=64)
             xsc = work.tile([P, HALF * P], U8, name="xsc", tag="xsc", align_bytes=64)
-            nc.vector.quantize_mx(out=xc[:].bitcast(FP8X4), scales=xsc[:], in_=grp[:])
+            nc.vector.quantize_mx(out=xc[:].bitcast(FP8X4), scales=xsc[:], in_=st[("grp", unit)][:])
             ss = small.tile([P, HALF], F32, name="ss", tag="ss")
-            ys = []
-            for a in range(HALF):
-                yp = psum.tile([P, D], F32, name="yp", tag="mm", bufs=3)
-                nc.tensor.matmul_mx(
-                    out=yp[:],
-                    lhsT=xc[:, a * P : (a + 1) * P].bitcast(FP8X4),
-                    lhsT_scale=xsc[:, a * P : (a + 1) * P],
-                    rhs=wcodes[side][:].bitcast(FP8X4),
-                    rhs_scale=wscl[side][:],
-                    start=True,
-                    stop=True,
-                )
-                y = work.tile([P, D], F32, name="y", tag="y", bufs=6)
-                nc.vector.tensor_tensor(out=y[:], in0=yp[:], in1=bias_b[side][:], op=ALU.add)
-                sq = work.tile([P, D], BF16, name="sq", tag="sq", bufs=1)
-                nc.scalar.activation(out=sq[:], in_=y[:], func=ACT.Square, accum_out=ss[:, a : a + 1])
-                ys.append(y)
+            st[("xc", unit)] = (xc, xsc, ss)
+
+        def project(unit, a):
+            side = unit[1]
+            xc, xsc, ss = st[("xc", unit)]
+            yp = psum.tile([P, D], F32, name="yp", tag="mm", bufs=4)
+            nc.tensor.matmul_mx(
+                out=yp[:],
+                lhsT=xc[:, a * P : (a + 1) * P].bitcast(FP8X4),
+                lhsT_scale=xsc[:, a * P : (a + 1) * P],
+                rhs=wcodes[side][:].bitcast(FP8X4),
+                rhs_scale=wscl[side][:],
+                start=True,
+                stop=True,
+            )
+            y = work.tile([P, D], F32, name="y", tag="y", bufs=8)
+            nc.vector.tensor_tensor(out=y[:], in0=yp[:], in1=bias_b[side][:], op=ALU.add)
+            sq = work.tile([P, D], BF16, name="sq", tag="sq", bufs=1)
+            nc.scalar.activation(out=sq[:], in_=y[:], func=ACT.Square, accum_out=ss[:, a : a + 1])
+            st[("y", unit, a)] = y
+
+        def normalise(unit):
+            ss = st[("xc", unit)][2]
             ssc = small.tile([P, HALF], F32, name="ssc", tag="ssc")
-            nc.gpsimd.tensor_scalar(out=ssc[:], in0=ss[:], scalar1=1e-24, scalar2=0.0, op0=ALU.max, op1=ALU.add)
+            nc.vector.tensor_scalar_max(out=ssc[:], in0=ss[:], scalar1=1e-24)
             rn = small.tile([P, HALF], F32, name="rn", tag="rn")
             nc.gpsimd.tensor_tensor(out=rn[:], in0=ssc[:], in1=mhalf[:], op=ALU.pow)
             qh = work.tile([P, HALF * D], BF16, name="qh", tag="qh")
             for a in range(HALF):
-                nc.vector.tensor_scalar(
+                nc.gpsimd.tensor_scalar(
                     out=qh[:, a * D : (a + 1) * D],
-                    in0=ys[a][:],
+                    in0=st[("y", unit, a)][:],
                     scalar1=rn[:, a : a + 1],
-                    scalar2=None,
+                    scalar2=0.0,
                     op0=ALU.mult,
+                    op1=ALU.add,
                 )
+            st[("qh", unit)] = qh
+
+        def turn_rows(unit):
             qg = work.tile([P, HALF * P * 4], BF16, name="grp", tag="grp", align_bytes=64)
-            words_to_groups(qh[:].bitcast(F32), qg[:].bitcast(F32), nc.scalar.copy)
+            words_to_groups(st[("qh", unit)][:].bitcast(F32), qg[:].bitcast(F32), nc.scalar.copy)
+            st[("qg", unit)] = qg
+
+        def quant_rows(unit):
+            b, side, h = unit
             nc.vector.quantize_mx(
                 out=codes[(side, b)][:, h * 512 : (h + 1) * 512].bitcast(FP8X4),
                 scales=scl[(side, b)][:, h * 512 : (h + 1) * 512],
-                in_=qg[:],
+                in_=st[("qg", unit)][:],
             )
 
+        def open_codes(b):
+            for side in range(2):
+                codes[(side, b)] = cpool.tile([P, T], U32, name="c%d" % side, align_bytes=64)
+                scl[(side, b)] = cpool.tile([P, T], U8, name="s%d" % side, align_bytes=64)
+
         def s_pass(b, it, hh):
-            sp = psum.tile([P, 512], F32, name="sp", tag="mm", bufs=3)
+            sp = psum.tile([P, 512], F32, name="sp", tag="mm", bufs=4)
             nc.tensor.matmul_mx(
                 out=sp[:],
                 lhsT=codes[(0, b)][:, it * P : (it + 1) * P].bitcast(FP8X4),
@@ -149,21 +178,36 @@ def tile_sinkhornot_t_kernel(tc, drone_tokens, sat_tokens, Wq, bq, Wk, bk, out_0
             )
             return sp
 
-        def fill(b, it, kh, kl, kth, ktl, r0):
-            e = work.tile([P, T], F32, name="e", tag="e", bufs=3)
-            for hh in range(2):
-                sp = s_pass(b, it, hh)
-                nc.scalar.activation(
-                    out=e[:, hh * 512 : (hh + 1) * 512],
-                    in_=sp[:],
-                    func=ACT.Exp,
-                    scale=10.0,
-                    accum_out=r0[:, it * 2 + hh : it * 2 + hh + 1],
-                )
+        km = {}
+
+        def open_k(b):
+            km[b] = []
+            for part in ("kh", "kl", "kth", "ktl"):
+                kt = kpool.tile([P, NT * T], BF16, name=part)
+                km[b].append(kt)
+            st[("r0", b)] = small.tile([P, NT, 2], F32, name="r0", tag="r0")
+
+        def fill_exp(b, it, hh):
+            if hh == 0:
+                st[("e", b, it)] = work.tile([P, T], F32, name="e", tag="e", bufs=3)
+            sp = s_pass(b, it, hh)
+            nc.scalar.activation(
+                out=st[("e", b, it)][:, hh * 512 : (hh + 1) * 512],
+                in_=sp[:],
+                func=ACT.Exp,
+                scale=10.0,
+                accum_out=st[("r0", b)][:, it, hh : hh + 1],
+            )
+
+        def fill_split(b, it):
+            kh, kl = km[b][:2]
+            e = st[("e", b, it)]
             cols = slice(it * T, (it + 1) * T)
             nc.vector.tensor_copy(out=kh[:, cols], in_=e[:])
             nc.vector.tensor_tensor(out=kl[:, cols], in0=e[:], in1=kh[:, cols], op=ALU.subtract)
-            for k, kt in ((kh, kth), (kl, ktl)):
+
+        def fill_turn(b, it):
+            for k, kt in ((km[b][0], km[b][2]), (km[b][1], km[b][3])):
                 tb = psum.tile([P, T], BF16, name="tb", tag="tr", bufs=3)
                 for jt in range(NT):
                     nc.tensor.transpose(
@@ -171,24 +215,26 @@ def tile_sinkhornot_t_kernel(tc, drone_tokens, sat_tokens, Wq, bq, Wk, bk, out_0
                         in_=k[:, it * T + jt * P : it * T + (jt + 1) * P],
                         identity=ident_b[:],
                     )
-                nc.scalar.copy(out=kt[:, cols], in_=tb[:])
+                nc.scalar.copy(out=kt[:, it * T : (it + 1) * T], in_=tb[:])
 
         def inverse(sums):
             c8 = small.tile([P, NT], F32, name="c8", tag="c8")
             nc.vector.tensor_reduce(out=c8[:], in_=sums, axis=AX.X, op=ALU.add)
-            v8 = small.tile([P, NT], F32, name="v8", tag="v8", bufs=8)
-            nc.gpsimd.tensor_tensor(out=v8[:], in0=c8[:], in1=mone[:], op=ALU.pow)
             vp = small.tile([P, NT, 2], BF16, name="vp", tag="vp")
-            nc.gpsimd.tensor_copy(out=vp[:, :, 0], in_=v8[:])
-            nc.gpsimd.tensor_tensor(out=vp[:, :, 1], in0=v8[:], in1=vp[:, :, 0], op=ALU.subtract)
+            with nc.allow_low_precision(reason="the second part carries what this rounding leaves"):
+                nc.vector.reciprocal(out=vp[:, :, 0], in_=c8[:])
+            v8 = small.tile([P, NT], F32, name="v8", tag="v8", bufs=8)
+            nc.vector.reciprocal(out=v8[:], in_=c8[:])
+            nc.vector.tensor_tensor(out=vp[:, :, 1], in0=v8[:], in1=vp[:, :, 0], op=ALU.subtract)
             return v8, vp
 
-        def matvec(kh, kl, vp, rows):
-            mv = psum.tile([P, NT, 2], F32, name="mv", tag="mv")
+        def matvec(b, rows, vp, between):
+            k2 = km[b][2:] if rows else km[b][:2]
+            mv = psum.tile([P, NT, 2], F32, name="mv", tag="mv", bufs=1)
             for o in range(NT):
                 for c in range(NT):
                     it, jt = (o, c) if rows else (c, o)
-                    for i, k in enumerate((kh, kl)):
+                    for i, k in enumerate(k2):
                         nc.tensor.matmul(
                             out=mv[:, o, :],
                             lhsT=k[:, it * T + jt * P : it * T + (jt + 1) * P],
@@ -196,9 +242,21 @@ def tile_sinkhornot_t_kernel(tc, drone_tokens, sat_tokens, Wq, bq, Wk, bk, out_0
                             start=(c == 0 and i == 0),
                             stop=(c == NT - 1 and i == 1),
                         )
+                for call in between[o * len(between) // NT : (o + 1) * len(between) // NT]:
+                    call()
             return mv
 
-        def finish(b, u8, v8):
+        uv = {}
+
+        def half_step(b, n, between):
+            if n == 0:
+                uv[(b, 0)] = inverse(st[("r0", b)][:])
+            rows = n % 2 == 1
+            mv = matvec(b, rows, uv[(b, 1 if rows else 0)][1], between)
+            uv[(b, 0 if rows else 1)] = inverse(mv[:])
+
+        def spread(b):
+            v8 = uv[(b, 1)][0]
             vb = work.tile([P, T], F32, name="vb", tag="vb", bufs=1)
             for hh in range(2):
                 vbp = psum.tile([P, 512], F32, name="vbp", tag="tr", bufs=3)
@@ -210,56 +268,108 @@ def tile_sinkhornot_t_kernel(tc, drone_tokens, sat_tokens, Wq, bq, Wk, bk, out_0
                         identity=ident_f[:],
                     )
                 nc.scalar.copy(out=vb[:, hh * 512 : (hh + 1) * 512], in_=vbp[:])
-            ov = out_0[b].rearrange("(p n) j -> p n j", n=NT)
-            for it in range(NT):
-                e = work.tile([P, T], F32, name="e", tag="e", bufs=3)
-                sps = []
-                for hh in range(2):
-                    sp = s_pass(b, it, hh)
-                    nc.scalar.activation(out=e[:, hh * 512 : (hh + 1) * 512], in_=sp[:], func=ACT.Exp, scale=10.0)
-                    sps.append(sp)
+            st[("vb", b)] = vb
+
+        def plan_exp(b, it, hh):
+            if hh == 0:
+                st[("e", b, it)] = work.tile([P, T], F32, name="e", tag="e", bufs=3)
+                st[("sp", b, it)] = []
+            sp = s_pass(b, it, hh)
+            st[("sp", b, it)].append(sp)
+            nc.scalar.activation(
+                out=st[("e", b, it)][:, hh * 512 : (hh + 1) * 512], in_=sp[:], func=ACT.Exp, scale=10.0
+            )
+
+        def plan_store(b, it):
+            e = st[("e", b, it)]
+            u8 = uv[(b, 0)][0]
+            nc.vector.scalar_tensor_tensor(
+                out=e[:], in0=e[:], scalar=u8[:, it : it + 1], in1=st[("vb", b)][:], op0=ALU.mult, op1=ALU.mult
+            )
+            for hh in range(2):
+                junk = work.tile([P, 512], F32, name="junk", tag="junk", bufs=1)
+                col = (b * NT + it) * 2 + hh
                 nc.vector.scalar_tensor_tensor(
-                    out=e[:], in0=e[:], scalar=u8[:, it : it + 1], in1=vb[:], op0=ALU.mult, op1=ALU.mult
+                    out=junk[:],
+                    in0=st[("sp", b, it)][hh][:],
+                    scalar=1.0,
+                    in1=e[:, hh * 512 : (hh + 1) * 512],
+                    op0=ALU.subtract,
+                    op1=ALU.mult,
+                    accum_out=ota[:, col : col + 1],
                 )
-                for hh in range(2):
-                    junk = work.tile([P, 512], F32, name="junk", tag="junk", bufs=1)
-                    col = (b * NT + it) * 2 + hh
-                    nc.vector.scalar_tensor_tensor(
-                        out=junk[:],
-                        in0=sps[hh][:],
-                        scalar=1.0,
-                        in1=e[:, hh * 512 : (hh + 1) * 512],
-                        op0=ALU.subtract,
-                        op1=ALU.mult,
-                        accum_out=ota[:, col : col + 1],
-                    )
-                nc.sync.dma_start(out=ov[:, it, :], in_=e[:])
+            nc.sync.dma_start(out=out_0[b].rearrange("(p n) j -> p n j", n=NT)[:, it, :], in_=e[:])
 
+        unit_at = {}
+        fill_at = {}
+        step_at = {}
+        spread_at = {}
+        plan_at = {}
+        last = 0
         for b in range(B):
-            for side in range(2):
-                codes[(side, b)] = cpool.tile([P, T], U32, name="c%d" % side, align_bytes=64)
-                scl[(side, b)] = cpool.tile([P, T], U8, name="s%d" % side, align_bytes=64)
-            for side in (1, 0):
-                for h in range(2):
-                    project(b, side, h)
-            kh = kpool.tile([P, NT * T], BF16, name="kh")
-            kl = kpool.tile([P, NT * T], BF16, name="kl")
-            kth = kpool.tile([P, NT * T], BF16, name="kth")
-            ktl = kpool.tile([P, NT * T], BF16, name="ktl")
-            r0 = small.tile([P, NT, 2], F32, name="r0", tag="r0")
-            r0f = r0[:].rearrange("p n c -> p (n c)")
+            m0 = FIRST_STEP + STEPS * b
+            order = [(b, 1, 0), (b, 1, 1), (b, 0, 0), (b, 0, 1)]
+            for i, unit in enumerate(order):
+                unit_at[i if b == 0 else m0 - 14 + 2 * i] = unit
             for it in range(NT):
-                fill(b, it, kh, kl, kth, ktl, r0f)
-            u8, up = inverse(r0[:])
-            for step in range(ITERS):
-                if step > 0:
-                    mv = matvec(kth, ktl, vp, True)
-                    u8, up = inverse(mv[:])
-                mv = matvec(kh, kl, up, False)
-                v8, vp = inverse(mv[:])
-            finish(b, u8, v8)
+                t = m0 - 4 + it // 2 if b == 0 else m0 - 6 + it * 6 // NT
+                fill_at.setdefault(t, []).append((b, it))
+            for n in range(STEPS):
+                step_at[m0 + n] = (b, n)
+            spread_at[m0 + STEPS] = b
+            for it in range(NT):
+                t = m0 + STEPS + 1 + (it if b < B - 1 else it // 2)
+                plan_at.setdefault(t, []).append((b, it))
+                last = max(last, t)
 
-        tp = psum.tile([P, B * NT * 2], F32, name="tp", tag="mv")
+        for side, w in ((1, Wk), (0, Wq)):
+            weights(side, w)
+        for t in range(2):
+            if t in unit_at:
+                load(unit_at[t])
+        for t in range(last + 1):
+            if t + 2 in unit_at:
+                load(unit_at[t + 2])
+            if t - 4 in unit_at:
+                unit = unit_at[t - 4]
+                if unit[0] not in [k[1] for k in codes]:
+                    open_codes(unit[0])
+                quant_rows(unit)
+            if t - 1 in unit_at:
+                quant_tokens(unit_at[t - 1])
+            if t - 2 in unit_at:
+                normalise(unit_at[t - 2])
+            mx = []
+            if t - 1 in unit_at:
+                for a in range(HALF):
+                    mx.append(lambda u=unit_at[t - 1], a=a: project(u, a))
+            for b, it in fill_at.get(t, []):
+                if it == 0:
+                    open_k(b)
+                for hh in range(2):
+                    mx.append(lambda b=b, it=it, hh=hh: fill_exp(b, it, hh))
+            for b, it in plan_at.get(t, []):
+                for hh in range(2):
+                    mx.append(lambda b=b, it=it, hh=hh: plan_exp(b, it, hh))
+            if t in step_at:
+                half_step(step_at[t][0], step_at[t][1], mx)
+            else:
+                for call in mx:
+                    call()
+            if t - 3 in unit_at:
+                turn_rows(unit_at[t - 3])
+            if t in unit_at:
+                turn_tokens(unit_at[t])
+            for b, it in fill_at.get(t - 1, []):
+                fill_turn(b, it)
+            if t in spread_at:
+                spread(spread_at[t])
+            for b, it in fill_at.get(t, []):
+                fill_split(b, it)
+            for b, it in plan_at.get(t, []):
+                plan_store(b, it)
+
+        tp = psum.tile([P, B * NT * 2], F32, name="tp", tag="mv", bufs=1)
         nc.tensor.matmul(out=tp[:], lhsT=ones_f[:], rhs=ota[:], start=True, stop=True)
         tot = small.tile([P, 1], F32, name="tot", tag="tot")
         nc.vector.tensor_reduce(out=tot[:], in_=tp[:], axis=AX.X, op=ALU.add)

@@ -18,9 +18,12 @@ T = 1024
 D = 512
 NT = T // P
 HALF = 4
+NH = NT // 2
+COLS = 5
 ITERS = 5
 STEPS = 2 * ITERS - 1
-FIRST_STEP = 11
+FIRST_STEP = 12
+SPACING = 9
 
 FLOPS = 2 * 2 * B * T * D * D + 2 * B * T * T * D
 
@@ -50,14 +53,19 @@ def tile_sinkhornot_t_kernel(tc, drone_tokens, sat_tokens, Wq, bq, Wk, bk, out_0
         mhalf = keep.tile([P, HALF], F32, name="mhalf")
         nc.vector.memset(mhalf[:], -0.5)
         ota = keep.tile([P, B * NT * 2], F32, name="ota")
+        vps_all = []
+        for i in range(8):
+            vp = keep.tile([P, NH, COLS], BF16, name="vp%d" % i)
+            nc.vector.memset(vp[:], 0.0)
+            vps_all.append(vp)
 
         wcodes = [keep.tile([P, D], U32, name="wc%d" % s, align_bytes=64) for s in range(2)]
         wscl = [keep.tile([P, D], U8, name="ws%d" % s, align_bytes=64) for s in range(2)]
         codes = {}
         scl = {}
 
-        def words_to_groups(src_f, grp_f, copy):
-            for pair in range(2):
+        def words_to_groups(src_f, grp_f, copy, pairs=(0, 1)):
+            for pair in pairs:
                 xt = psum.tile([P, 512], F32, name="xt", tag="tr", bufs=3)
                 for a in range(2):
                     n = pair * 2 + a
@@ -71,6 +79,18 @@ def tile_sinkhornot_t_kernel(tc, drone_tokens, sat_tokens, Wq, bq, Wk, bk, out_0
                     out=grp_f[:, pair * 512 : (pair + 1) * 512].rearrange("p (a r u) -> p a r u", a=2, u=2),
                     in_=xt[:].rearrange("p (a u r) -> p a r u", a=2, u=2),
                 )
+
+        def spare():
+            sp = psum.tile([P, D], F32, name="spare", tag="mm", bufs=3)
+            nc.tensor.matmul_mx(
+                out=sp[:],
+                lhsT=wcodes[0][:, 0:P].bitcast(FP8X4),
+                lhsT_scale=wscl[0][:, 0:P],
+                rhs=wcodes[1][:].bitcast(FP8X4),
+                rhs_scale=wscl[1][:],
+                start=True,
+                stop=True,
+            )
 
         def weights(side, w):
             raw = work.tile([P, 4 * D], BF16, name="xs", tag="xs", bufs=3)
@@ -98,10 +118,12 @@ def tile_sinkhornot_t_kernel(tc, drone_tokens, sat_tokens, Wq, bq, Wk, bk, out_0
                 )
             st[("xs", unit)] = xs
 
-        def turn_tokens(unit):
-            grp = work.tile([P, HALF * P * 4], BF16, name="grp", tag="grp", align_bytes=64)
-            words_to_groups(st[("xs", unit)][:].bitcast(F32), grp[:].bitcast(F32), nc.scalar.copy)
-            st[("grp", unit)] = grp
+        def turn_tokens(unit, pair):
+            if pair == 0:
+                st[("grp", unit)] = work.tile([P, HALF * P * 4], BF16, name="grp", tag="grp", align_bytes=64)
+            words_to_groups(
+                st[("xs", unit)][:].bitcast(F32), st[("grp", unit)][:].bitcast(F32), nc.scalar.copy, (pair,)
+            )
 
         def quant_tokens(unit):
             xc = work.tile([P, HALF * P], U32, name="xc", tag="xc", align_bytes=64)
@@ -113,7 +135,7 @@ def tile_sinkhornot_t_kernel(tc, drone_tokens, sat_tokens, Wq, bq, Wk, bk, out_0
         def project(unit, a):
             side = unit[1]
             xc, xsc, ss = st[("xc", unit)]
-            yp = psum.tile([P, D], F32, name="yp", tag="mm", bufs=4)
+            yp = psum.tile([P, D], F32, name="yp", tag="mm", bufs=3)
             nc.tensor.matmul_mx(
                 out=yp[:],
                 lhsT=xc[:, a * P : (a + 1) * P].bitcast(FP8X4),
@@ -147,13 +169,17 @@ def tile_sinkhornot_t_kernel(tc, drone_tokens, sat_tokens, Wq, bq, Wk, bk, out_0
                 )
             st[("qh", unit)] = qh
 
-        def turn_rows(unit):
-            qg = work.tile([P, HALF * P * 4], BF16, name="grp", tag="grp", align_bytes=64)
-            words_to_groups(st[("qh", unit)][:].bitcast(F32), qg[:].bitcast(F32), nc.scalar.copy)
-            st[("qg", unit)] = qg
+        def turn_rows(unit, pair):
+            if pair == 0:
+                st[("qg", unit)] = work.tile([P, HALF * P * 4], BF16, name="grp", tag="grp", align_bytes=64)
+            words_to_groups(
+                st[("qh", unit)][:].bitcast(F32), st[("qg", unit)][:].bitcast(F32), nc.scalar.copy, (pair,)
+            )
 
         def quant_rows(unit):
             b, side, h = unit
+            if (side, b) not in codes:
+                open_codes(b)
             nc.vector.quantize_mx(
                 out=codes[(side, b)][:, h * 512 : (h + 1) * 512].bitcast(FP8X4),
                 scales=scl[(side, b)][:, h * 512 : (h + 1) * 512],
@@ -165,8 +191,8 @@ def tile_sinkhornot_t_kernel(tc, drone_tokens, sat_tokens, Wq, bq, Wk, bk, out_0
                 codes[(side, b)] = cpool.tile([P, T], U32, name="c%d" % side, align_bytes=64)
                 scl[(side, b)] = cpool.tile([P, T], U8, name="s%d" % side, align_bytes=64)
 
-        def s_pass(b, it, hh):
-            sp = psum.tile([P, 512], F32, name="sp", tag="mm", bufs=4)
+        def s_pass(b, it, hh, tag):
+            sp = psum.tile([P, 512], F32, name="sp", tag=tag, bufs=3)
             nc.tensor.matmul_mx(
                 out=sp[:],
                 lhsT=codes[(0, b)][:, it * P : (it + 1) * P].bitcast(FP8X4),
@@ -190,7 +216,7 @@ def tile_sinkhornot_t_kernel(tc, drone_tokens, sat_tokens, Wq, bq, Wk, bk, out_0
         def fill_exp(b, it, hh):
             if hh == 0:
                 st[("e", b, it)] = work.tile([P, T], F32, name="e", tag="e", bufs=3)
-            sp = s_pass(b, it, hh)
+            sp = s_pass(b, it, hh, "mm")
             nc.scalar.activation(
                 out=st[("e", b, it)][:, hh * 512 : (hh + 1) * 512],
                 in_=sp[:],
@@ -206,54 +232,69 @@ def tile_sinkhornot_t_kernel(tc, drone_tokens, sat_tokens, Wq, bq, Wk, bk, out_0
             nc.vector.tensor_copy(out=kh[:, cols], in_=e[:])
             nc.vector.tensor_tensor(out=kl[:, cols], in0=e[:], in1=kh[:, cols], op=ALU.subtract)
 
-        def fill_turn(b, it):
-            for k, kt in ((km[b][0], km[b][2]), (km[b][1], km[b][3])):
-                tb = psum.tile([P, T], BF16, name="tb", tag="tr", bufs=3)
-                for jt in range(NT):
-                    nc.tensor.transpose(
-                        out=tb[:, jt * P : (jt + 1) * P],
-                        in_=k[:, it * T + jt * P : it * T + (jt + 1) * P],
-                        identity=ident_b[:],
-                    )
-                nc.scalar.copy(out=kt[:, it * T : (it + 1) * T], in_=tb[:])
+        def fill_turn(b, it, part):
+            k, kt = km[b][part], km[b][part + 2]
+            tb = psum.tile([P, T], BF16, name="tb", tag="tr", bufs=3)
+            for jt in range(NT):
+                nc.tensor.transpose(
+                    out=tb[:, jt * P : (jt + 1) * P],
+                    in_=k[:, it * T + jt * P : it * T + (jt + 1) * P],
+                    identity=ident_b[:],
+                )
+            nc.scalar.copy(out=kt[:, it * T : (it + 1) * T], in_=tb[:])
 
-        def inverse(sums):
-            c8 = small.tile([P, NT], F32, name="c8", tag="c8")
-            nc.vector.tensor_reduce(out=c8[:], in_=sums, axis=AX.X, op=ALU.add)
-            vp = small.tile([P, NT, 2], BF16, name="vp", tag="vp")
+        def inverse(sums, v8, h):
+            c4 = small.tile([P, NH], F32, name="c4", tag="c4", bufs=4)
+            nc.vector.tensor_reduce(out=c4[:], in_=sums, axis=AX.X, op=ALU.add)
+            vp = vps_all[turn[0] % len(vps_all)]
+            turn[0] += 1
             with nc.allow_low_precision(reason="the second part carries what this rounding leaves"):
-                nc.vector.reciprocal(out=vp[:, :, 0], in_=c8[:])
-            v8 = small.tile([P, NT], F32, name="v8", tag="v8", bufs=8)
-            nc.vector.reciprocal(out=v8[:], in_=c8[:])
-            nc.vector.tensor_tensor(out=vp[:, :, 1], in0=v8[:], in1=vp[:, :, 0], op=ALU.subtract)
-            return v8, vp
-
-        def matvec(b, rows, vp, between):
-            k2 = km[b][2:] if rows else km[b][:2]
-            mv = psum.tile([P, NT, 2], F32, name="mv", tag="mv", bufs=1)
-            for o in range(NT):
-                for c in range(NT):
-                    it, jt = (o, c) if rows else (c, o)
-                    for i, k in enumerate(k2):
-                        nc.tensor.matmul(
-                            out=mv[:, o, :],
-                            lhsT=k[:, it * T + jt * P : it * T + (jt + 1) * P],
-                            rhs=vp[:, c, :],
-                            start=(c == 0 and i == 0),
-                            stop=(c == NT - 1 and i == 1),
-                        )
-                for call in between[o * len(between) // NT : (o + 1) * len(between) // NT]:
-                    call()
-            return mv
+                nc.vector.reciprocal(out=vp[:, :, 0], in_=c4[:])
+            cols = slice(h * NH, (h + 1) * NH)
+            nc.vector.reciprocal(out=v8[:, cols], in_=c4[:])
+            nc.vector.tensor_tensor(out=vp[:, :, 1], in0=v8[:, cols], in1=vp[:, :, 0], op=ALU.subtract)
+            return vp
 
         uv = {}
+        turn = [0]
 
         def half_step(b, n, between):
             if n == 0:
-                uv[(b, 0)] = inverse(st[("r0", b)][:])
+                u8 = small.tile([P, NT], F32, name="v8", tag="v8", bufs=8)
+                r0 = st[("r0", b)]
+                ups = []
+                for h in range(2):
+                    ups.append(inverse(r0[:, h * NH : (h + 1) * NH, :], u8, h))
+                uv[(b, 0)] = (u8, ups)
             rows = n % 2 == 1
-            mv = matvec(b, rows, uv[(b, 1 if rows else 0)][1], between)
-            uv[(b, 0 if rows else 1)] = inverse(mv[:])
+            k2 = km[b][2:] if rows else km[b][:2]
+            vps = uv[(b, 1 if rows else 0)][1]
+            mvs = []
+            for h in range(2):
+                mv = psum.tile([P, NH, 2, COLS], F32, name="mv", tag="mv%d" % h, bufs=1)
+                mvs.append(mv)
+            v8 = small.tile([P, NT], F32, name="v8", tag="v8", bufs=8)
+            new = []
+            slot = 0
+            for s in range(2):
+                for o in range(NT):
+                    for c in range(NH):
+                        it, jt = (o, s * NH + c) if rows else (s * NH + c, o)
+                        for i, k in enumerate(k2):
+                            nc.tensor.matmul(
+                                out=mvs[o // NH][:, o % NH, s, :],
+                                lhsT=k[:, it * T + jt * P : it * T + (jt + 1) * P],
+                                rhs=vps[s][:, c, :],
+                                start=(c == 0 and i == 0),
+                                stop=(c == NH - 1 and i == 1),
+                            )
+                    for call in between[slot * len(between) // 16 : (slot + 1) * len(between) // 16]:
+                        call()
+                    slot += 1
+                    if s == 1 and o % NH == NH - 1:
+                        h = o // NH
+                        new.append(inverse(mvs[h][:].rearrange("p o s n -> p o (s n)"), v8, h))
+            uv[(b, 0 if rows else 1)] = (v8, new)
 
         def spread(b):
             v8 = uv[(b, 1)][0]
@@ -274,7 +315,7 @@ def tile_sinkhornot_t_kernel(tc, drone_tokens, sat_tokens, Wq, bq, Wk, bk, out_0
             if hh == 0:
                 st[("e", b, it)] = work.tile([P, T], F32, name="e", tag="e", bufs=3)
                 st[("sp", b, it)] = []
-            sp = s_pass(b, it, hh)
+            sp = s_pass(b, it, hh, "tr" if b == B - 1 and it % 2 else "mm")
             st[("sp", b, it)].append(sp)
             nc.scalar.activation(
                 out=st[("e", b, it)][:, hh * 512 : (hh + 1) * 512], in_=sp[:], func=ACT.Exp, scale=10.0
@@ -307,18 +348,17 @@ def tile_sinkhornot_t_kernel(tc, drone_tokens, sat_tokens, Wq, bq, Wk, bk, out_0
         plan_at = {}
         last = 0
         for b in range(B):
-            m0 = FIRST_STEP + STEPS * b
+            m0 = FIRST_STEP + SPACING * b
             order = [(b, 1, 0), (b, 1, 1), (b, 0, 0), (b, 0, 1)]
             for i, unit in enumerate(order):
-                unit_at[i if b == 0 else m0 - 14 + 2 * i] = unit
+                unit_at[i if b == 0 else m0 - 12 + i] = unit
             for it in range(NT):
-                t = m0 - 4 + it // 2 if b == 0 else m0 - 6 + it * 6 // NT
-                fill_at.setdefault(t, []).append((b, it))
+                fill_at.setdefault(m0 - 4 + it // 2, []).append((b, it))
             for n in range(STEPS):
-                step_at[m0 + n] = (b, n)
+                step_at.setdefault(m0 + n, []).append((b, n))
             spread_at[m0 + STEPS] = b
             for it in range(NT):
-                t = m0 + STEPS + 1 + (it if b < B - 1 else it // 2)
+                t = m0 + STEPS + 1 + it
                 plan_at.setdefault(t, []).append((b, it))
                 last = max(last, t)
 
@@ -330,46 +370,64 @@ def tile_sinkhornot_t_kernel(tc, drone_tokens, sat_tokens, Wq, bq, Wk, bk, out_0
         for t in range(last + 1):
             if t + 2 in unit_at:
                 load(unit_at[t + 2])
-            if t - 4 in unit_at:
-                unit = unit_at[t - 4]
-                if unit[0] not in [k[1] for k in codes]:
-                    open_codes(unit[0])
-                quant_rows(unit)
-            if t - 1 in unit_at:
-                quant_tokens(unit_at[t - 1])
-            if t - 2 in unit_at:
-                normalise(unit_at[t - 2])
-            mx = []
-            if t - 1 in unit_at:
-                for a in range(HALF):
-                    mx.append(lambda u=unit_at[t - 1], a=a: project(u, a))
+            if t - 3 in unit_at:
+                normalise(unit_at[t - 3])
+            mx = [[], []]
             for b, it in fill_at.get(t, []):
                 if it == 0:
                     open_k(b)
                 for hh in range(2):
-                    mx.append(lambda b=b, it=it, hh=hh: fill_exp(b, it, hh))
+                    mx[0].append(lambda b=b, it=it, hh=hh: fill_exp(b, it, hh))
+            if t - 2 in unit_at:
+                for a in range(HALF):
+                    mx[a // 2].append(lambda u=unit_at[t - 2], a=a: project(u, a))
             for b, it in plan_at.get(t, []):
                 for hh in range(2):
-                    mx.append(lambda b=b, it=it, hh=hh: plan_exp(b, it, hh))
-            if t in step_at:
-                half_step(step_at[t][0], step_at[t][1], mx)
-            else:
-                for call in mx:
-                    call()
-            if t - 3 in unit_at:
-                turn_rows(unit_at[t - 3])
-            if t in unit_at:
-                turn_tokens(unit_at[t])
+                    mx[1].append(lambda b=b, it=it, hh=hh: plan_exp(b, it, hh))
+            turns = []
+            for pair in range(2):
+                if t - 4 in unit_at:
+                    turns.append(lambda u=unit_at[t - 4], pair=pair: turn_rows(u, pair))
+            for pair in range(2):
+                if t in unit_at:
+                    turns.append(lambda u=unit_at[t], pair=pair: turn_tokens(u, pair))
             for b, it in fill_at.get(t - 1, []):
-                fill_turn(b, it)
+                for part in range(2):
+                    turns.append(lambda b=b, it=it, part=part: fill_turn(b, it, part))
             if t in spread_at:
-                spread(spread_at[t])
+                turns.append(lambda b=spread_at[t]: spread(b))
+            late = [[], []]
+            if t - 1 in unit_at:
+                late[0].append(lambda u=unit_at[t - 1]: quant_tokens(u))
+            if t - 5 in unit_at:
+                late[0].append(lambda u=unit_at[t - 5]: quant_rows(u))
             for b, it in fill_at.get(t, []):
-                fill_split(b, it)
+                late[0].append(lambda b=b, it=it: fill_split(b, it))
             for b, it in plan_at.get(t, []):
-                plan_store(b, it)
+                late[1].append(lambda b=b, it=it: plan_store(b, it))
+            steps = step_at.get(t, [])
+            mx = mx[0] + mx[1]
+            late = late[0] + late[1]
+            if steps:
+                apart = len(turns) // 4 * 2
+                while len(mx) < apart + 5:
+                    mx.append(spare)
+                for i in range(2):
+                    (mx.pop(0) if len(mx) > apart + 5 else spare)()
+                half_step(steps[0][0], steps[0][1], mx[: len(mx) - apart])
+                rest = mx[len(mx) - apart :]
+                for i, call in enumerate(turns):
+                    call()
+                    if i % 4 == 1 and rest:
+                        rest.pop(0)()
+                        rest.pop(0)()
+            else:
+                for call in mx + turns:
+                    call()
+            for call in late:
+                call()
 
-        tp = psum.tile([P, B * NT * 2], F32, name="tp", tag="mv", bufs=1)
+        tp = psum.tile([P, B * NT * 2], F32, name="tp", tag="mv0", bufs=1)
         nc.tensor.matmul(out=tp[:], lhsT=ones_f[:], rhs=ota[:], start=True, stop=True)
         tot = small.tile([P, 1], F32, name="tot", tag="tot")
         nc.vector.tensor_reduce(out=tot[:], in_=tp[:], axis=AX.X, op=ALU.add)

@@ -31,7 +31,7 @@ FLOPS = 2 * 2 * B * T * D * D + 2 * B * T * T * D
 def tile_sinkhornot_t_kernel(tc, drone_tokens, sat_tokens, Wq, bq, Wk, bk, out_0, out_1):
     nc = tc.nc
     with ExitStack() as ctx:
-        ctx.enter_context(tc.manual_schedule())
+        ctx.enter_context(tc.manual_schedule(engines={mybir.EngineType.PE, mybir.EngineType.SP}))
         keep = ctx.enter_context(tc.tile_pool(name="keep", bufs=1))
         small = ctx.enter_context(tc.tile_pool(name="small", bufs=4))
         kpool = ctx.enter_context(tc.tile_pool(name="kpool", bufs=2))

@@ -19,7 +19,7 @@ D = 512
 NT = T // P
 HALF = 4
 NH = NT // 2
-COLS = 5
+COLS = 4
 ITERS = 5
 STEPS = 2 * ITERS - 1
 FIRST_STEP = 12
@@ -66,7 +66,7 @@ def tile_sinkhornot_t_kernel(tc, drone_tokens, sat_tokens, Wq, bq, Wk, bk, out_0
 
         def words_to_groups(src_f, grp_f, copy, pairs=(0, 1)):
             for pair in pairs:
-                xt = psum.tile([P, 512], F32, name="xt", tag="tr", bufs=3)
+                xt = psum.tile([P, 512], F32, name="xt", tag="mm", bufs=8)
                 for a in range(2):
                     n = pair * 2 + a
                     for u in range(2):
@@ -81,7 +81,7 @@ def tile_sinkhornot_t_kernel(tc, drone_tokens, sat_tokens, Wq, bq, Wk, bk, out_0
                 )
 
         def spare():
-            sp = psum.tile([P, D], F32, name="spare", tag="mm", bufs=3)
+            sp = psum.tile([P, D], F32, name="spare", tag="mm", bufs=8)
             nc.tensor.matmul_mx(
                 out=sp[:],
                 lhsT=wcodes[0][:, 0:P].bitcast(FP8X4),
@@ -135,7 +135,7 @@ def tile_sinkhornot_t_kernel(tc, drone_tokens, sat_tokens, Wq, bq, Wk, bk, out_0
         def project(unit, a):
             side = unit[1]
             xc, xsc, ss = st[("xc", unit)]
-            yp = psum.tile([P, D], F32, name="yp", tag="mm", bufs=3)
+            yp = psum.tile([P, D], F32, name="yp", tag="mm", bufs=8)
             nc.tensor.matmul_mx(
                 out=yp[:],
                 lhsT=xc[:, a * P : (a + 1) * P].bitcast(FP8X4),
@@ -159,13 +159,12 @@ def tile_sinkhornot_t_kernel(tc, drone_tokens, sat_tokens, Wq, bq, Wk, bk, out_0
             nc.gpsimd.tensor_tensor(out=rn[:], in0=ssc[:], in1=mhalf[:], op=ALU.pow)
             qh = work.tile([P, HALF * D], BF16, name="qh", tag="qh")
             for a in range(HALF):
-                nc.gpsimd.tensor_scalar(
+                nc.vector.tensor_scalar(
                     out=qh[:, a * D : (a + 1) * D],
                     in0=st[("y", unit, a)][:],
                     scalar1=rn[:, a : a + 1],
-                    scalar2=0.0,
+                    scalar2=None,
                     op0=ALU.mult,
-                    op1=ALU.add,
                 )
             st[("qh", unit)] = qh
 
@@ -191,8 +190,21 @@ def tile_sinkhornot_t_kernel(tc, drone_tokens, sat_tokens, Wq, bq, Wk, bk, out_0
                 codes[(side, b)] = cpool.tile([P, T], U32, name="c%d" % side, align_bytes=64)
                 scl[(side, b)] = cpool.tile([P, T], U8, name="s%d" % side, align_bytes=64)
 
+        def s_turned(b, jt, hh):
+            sp = psum.tile([P, 512], F32, name="sp", tag="mm", bufs=8)
+            nc.tensor.matmul_mx(
+                out=sp[:],
+                lhsT=codes[(1, b)][:, jt * P : (jt + 1) * P].bitcast(FP8X4),
+                lhsT_scale=scl[(1, b)][:, jt * P : (jt + 1) * P],
+                rhs=codes[(0, b)][:, hh * 512 : (hh + 1) * 512].bitcast(FP8X4),
+                rhs_scale=scl[(0, b)][:, hh * 512 : (hh + 1) * 512],
+                start=True,
+                stop=True,
+            )
+            return sp
+
         def s_pass(b, it, hh, tag):
-            sp = psum.tile([P, 512], F32, name="sp", tag=tag, bufs=3)
+            sp = psum.tile([P, 512], F32, name="sp", tag="mm", bufs=8)
             nc.tensor.matmul_mx(
                 out=sp[:],
                 lhsT=codes[(0, b)][:, it * P : (it + 1) * P].bitcast(FP8X4),
@@ -232,9 +244,14 @@ def tile_sinkhornot_t_kernel(tc, drone_tokens, sat_tokens, Wq, bq, Wk, bk, out_0
             nc.vector.tensor_copy(out=kh[:, cols], in_=e[:])
             nc.vector.tensor_tensor(out=kl[:, cols], in0=e[:], in1=kh[:, cols], op=ALU.subtract)
 
-        def fill_turn(b, it, part):
-            k, kt = km[b][part], km[b][part + 2]
-            tb = psum.tile([P, T], BF16, name="tb", tag="tr", bufs=3)
+        def fill_turned(b, jt, hh):
+            sp = s_turned(b, jt, hh)
+            lo = jt * T + hh * 512
+            nc.scalar.activation(out=km[b][2][:, lo : lo + 512], in_=sp[:], func=ACT.Exp, scale=10.0)
+
+        def fill_turn(b, it):
+            k, kt = km[b][1], km[b][3]
+            tb = psum.tile([P, T], BF16, name="tb", tag="mm", bufs=8)
             for jt in range(NT):
                 nc.tensor.transpose(
                     out=tb[:, jt * P : (jt + 1) * P],
@@ -271,7 +288,7 @@ def tile_sinkhornot_t_kernel(tc, drone_tokens, sat_tokens, Wq, bq, Wk, bk, out_0
             vps = uv[(b, 1 if rows else 0)][1]
             mvs = []
             for h in range(2):
-                mv = psum.tile([P, NH, 2, COLS], F32, name="mv", tag="mv%d" % h, bufs=1)
+                mv = psum.tile([P, NH, 2, COLS], F32, name="mv", tag="mm", bufs=8)
                 mvs.append(mv)
             v8 = small.tile([P, NT], F32, name="v8", tag="v8", bufs=8)
             new = []
@@ -281,9 +298,10 @@ def tile_sinkhornot_t_kernel(tc, drone_tokens, sat_tokens, Wq, bq, Wk, bk, out_0
                     for c in range(NH):
                         it, jt = (o, s * NH + c) if rows else (s * NH + c, o)
                         for i, k in enumerate(k2):
+                            lo = jt * T + it * P if rows and i == 0 else it * T + jt * P
                             nc.tensor.matmul(
                                 out=mvs[o // NH][:, o % NH, s, :],
-                                lhsT=k[:, it * T + jt * P : it * T + (jt + 1) * P],
+                                lhsT=k[:, lo : lo + P],
                                 rhs=vps[s][:, c, :],
                                 start=(c == 0 and i == 0),
                                 stop=(c == NH - 1 and i == 1),
@@ -300,7 +318,7 @@ def tile_sinkhornot_t_kernel(tc, drone_tokens, sat_tokens, Wq, bq, Wk, bk, out_0
             v8 = uv[(b, 1)][0]
             vb = work.tile([P, T], F32, name="vb", tag="vb", bufs=1)
             for hh in range(2):
-                vbp = psum.tile([P, 512], F32, name="vbp", tag="tr", bufs=3)
+                vbp = psum.tile([P, 512], F32, name="vbp", tag="mm", bufs=8)
                 for j in range(4):
                     jt = hh * 4 + j
                     nc.tensor.transpose(
@@ -343,6 +361,7 @@ def tile_sinkhornot_t_kernel(tc, drone_tokens, sat_tokens, Wq, bq, Wk, bk, out_0
 
         unit_at = {}
         fill_at = {}
+        turned_at = {}
         step_at = {}
         spread_at = {}
         plan_at = {}
@@ -354,6 +373,7 @@ def tile_sinkhornot_t_kernel(tc, drone_tokens, sat_tokens, Wq, bq, Wk, bk, out_0
                 unit_at[i if b == 0 else m0 - 12 + i] = unit
             for it in range(NT):
                 fill_at.setdefault(m0 - 4 + it // 2, []).append((b, it))
+                turned_at.setdefault(m0 - 3 + it // 2, []).append((b, it))
             for n in range(STEPS):
                 step_at.setdefault(m0 + n, []).append((b, n))
             spread_at[m0 + STEPS] = b
@@ -378,6 +398,9 @@ def tile_sinkhornot_t_kernel(tc, drone_tokens, sat_tokens, Wq, bq, Wk, bk, out_0
                     open_k(b)
                 for hh in range(2):
                     mx[0].append(lambda b=b, it=it, hh=hh: fill_exp(b, it, hh))
+            for b, jt in turned_at.get(t, []):
+                for hh in range(2):
+                    mx[1].append(lambda b=b, jt=jt, hh=hh: fill_turned(b, jt, hh))
             if t - 2 in unit_at:
                 for a in range(HALF):
                     mx[a // 2].append(lambda u=unit_at[t - 2], a=a: project(u, a))
@@ -392,8 +415,7 @@ def tile_sinkhornot_t_kernel(tc, drone_tokens, sat_tokens, Wq, bq, Wk, bk, out_0
                 if t in unit_at:
                     turns.append(lambda u=unit_at[t], pair=pair: turn_tokens(u, pair))
             for b, it in fill_at.get(t - 1, []):
-                for part in range(2):
-                    turns.append(lambda b=b, it=it, part=part: fill_turn(b, it, part))
+                turns.append(lambda b=b, it=it: fill_turn(b, it))
             if t in spread_at:
                 turns.append(lambda b=spread_at[t]: spread(b))
             late = [[], []]
@@ -427,7 +449,7 @@ def tile_sinkhornot_t_kernel(tc, drone_tokens, sat_tokens, Wq, bq, Wk, bk, out_0
             for call in late:
                 call()
 
-        tp = psum.tile([P, B * NT * 2], F32, name="tp", tag="mv0", bufs=1)
+        tp = psum.tile([P, B * NT * 2], F32, name="tp", tag="mm", bufs=8)
         nc.tensor.matmul(out=tp[:], lhsT=ones_f[:], rhs=ota[:], start=True, stop=True)
         tot = small.tile([P, 1], F32, name="tot", tag="tot")
         nc.vector.tensor_reduce(out=tot[:], in_=tp[:], axis=AX.X, op=ALU.add)

@@ -17,13 +17,16 @@ B = 4
 T = 1024
 D = 512
 NT = T // P
-HALF = 4
+PAIR = 2
+UNITS = NT // PAIR
 NH = NT // 2
 COLS = 4
+PASSES = ((0, (0, 1, 2, 3, 4, 5)), (1, (0, 1, 2, 3)), (0, (6, 7)), (1, (4, 5, 6, 7)))
 ITERS = 5
 STEPS = 2 * ITERS - 1
 FIRST_STEP = 12
-SPACING = 9
+WIDE = 7
+KICK = 2
 
 FLOPS = 2 * 2 * B * T * D * D + 2 * B * T * T * D
 
@@ -35,7 +38,7 @@ def tile_sinkhornot_t_kernel(tc, drone_tokens, sat_tokens, Wq, bq, Wk, bk, out_0
         keep = ctx.enter_context(tc.tile_pool(name="keep", bufs=1))
         small = ctx.enter_context(tc.tile_pool(name="small", bufs=4))
         kpool = ctx.enter_context(tc.tile_pool(name="kpool", bufs=2))
-        cpool = ctx.enter_context(tc.tile_pool(name="cpool", bufs=3))
+        cpool = ctx.enter_context(tc.tile_pool(name="cpool", bufs=4))
         work = ctx.enter_context(tc.tile_pool(name="work", bufs=2))
         psum = ctx.enter_context(tc.psum_pool(name="psum", bufs=2))
 
@@ -50,9 +53,11 @@ def tile_sinkhornot_t_kernel(tc, drone_tokens, sat_tokens, Wq, bq, Wk, bk, out_0
         make_identity(nc, ident_b[:])
         ones_f = keep.tile([P, P], F32, name="ones_f")
         nc.vector.memset(ones_f[:], 1.0)
-        mhalf = keep.tile([P, HALF], F32, name="mhalf")
+        mhalf = keep.tile([P, PAIR], F32, name="mhalf")
         nc.vector.memset(mhalf[:], -0.5)
         ota = keep.tile([P, B * NT * 2], F32, name="ota")
+        first = small.tile([P, 1], F32, name="first", tag="first", bufs=1)
+        nc.scalar.activation(out=first[:], in_=ones_f[:, 0:1], func=ACT.Exp)
         vps_all = []
         for i in range(8):
             vp = keep.tile([P, NH, COLS], BF16, name="vp%d" % i)
@@ -64,21 +69,19 @@ def tile_sinkhornot_t_kernel(tc, drone_tokens, sat_tokens, Wq, bq, Wk, bk, out_0
         codes = {}
         scl = {}
 
-        def words_to_groups(src_f, grp_f, copy, pairs=(0, 1)):
-            for pair in pairs:
-                xt = psum.tile([P, 512], F32, name="xt", tag="mm", bufs=8)
-                for a in range(2):
-                    n = pair * 2 + a
-                    for u in range(2):
-                        nc.tensor.transpose(
-                            out=xt[:, (a * 2 + u) * P : (a * 2 + u + 1) * P],
-                            in_=src_f[:, n * 256 + u * P : n * 256 + (u + 1) * P],
-                            identity=ident_f[:],
-                        )
-                copy(
-                    out=grp_f[:, pair * 512 : (pair + 1) * 512].rearrange("p (a r u) -> p a r u", a=2, u=2),
-                    in_=xt[:].rearrange("p (a u r) -> p a r u", a=2, u=2),
-                )
+        def words_to_groups(src_f, grp_f, copy):
+            xt = psum.tile([P, 512], F32, name="xt", tag="mm", bufs=8)
+            for a in range(PAIR):
+                for u in range(2):
+                    nc.tensor.transpose(
+                        out=xt[:, (a * 2 + u) * P : (a * 2 + u + 1) * P],
+                        in_=src_f[:, a * 256 + u * P : a * 256 + (u + 1) * P],
+                        identity=ident_f[:],
+                    )
+            copy(
+                out=grp_f.rearrange("p (a r u) -> p a r u", a=PAIR, u=2),
+                in_=xt[:].rearrange("p (a u r) -> p a r u", a=PAIR, u=2),
+            )
 
         def spare():
             sp = psum.tile([P, D], F32, name="spare", tag="mm", bufs=8)
@@ -92,44 +95,48 @@ def tile_sinkhornot_t_kernel(tc, drone_tokens, sat_tokens, Wq, bq, Wk, bk, out_0
                 stop=True,
             )
 
-        def weights(side, w):
-            raw = work.tile([P, 4 * D], BF16, name="xs", tag="xs", bufs=3)
+        def load_weights(w):
+            raw = work.tile([P, 4 * D], BF16, name="raw", tag="raw", bufs=2)
             nc.sync.dma_start(
                 out=raw[:].rearrange("p (n d) -> p n d", n=4), in_=w.rearrange("(n p) d -> p n d", p=P)
             )
-            grp = work.tile([P, HALF * P * 4], BF16, name="grp", tag="grp", align_bytes=64)
-            words_to_groups(raw[:].bitcast(F32), grp[:].bitcast(F32), nc.vector.tensor_copy)
-            nc.vector.quantize_mx(out=wcodes[side][:].bitcast(FP8X4), scales=wscl[side][:], in_=grp[:])
+            return raw
+
+        def weights(side, raw):
+            words = raw[:].bitcast(F32)
+            for i in range(2):
+                grp = work.tile([P, PAIR * P * 4], BF16, name="grp", tag="grp", bufs=4, align_bytes=64)
+                words_to_groups(words[:, i * 512 : (i + 1) * 512], grp[:].bitcast(F32), nc.vector.tensor_copy)
+                cols = slice(i * PAIR * P, (i + 1) * PAIR * P)
+                nc.vector.quantize_mx(out=wcodes[side][:, cols].bitcast(FP8X4), scales=wscl[side][:, cols], in_=grp[:])
 
         st = {}
 
         def load(unit):
             b, side, h = unit
-            xs = work.tile([P, HALF * D], BF16, name="xs", tag="xs", bufs=3)
+            xs = work.tile([P, PAIR * D], BF16, name="xs", tag="xs", bufs=4)
             if side == 0:
                 nc.sync.dma_start(
                     out=xs[:],
-                    in_=drone_tokens[b].rearrange("(p n) d -> p (n d)", n=NT)[:, h * HALF * D : (h + 1) * HALF * D],
+                    in_=drone_tokens[b].rearrange("(p n) d -> p (n d)", n=NT)[:, h * PAIR * D : (h + 1) * PAIR * D],
                 )
             else:
                 nc.sync.dma_start(
-                    out=xs[:].rearrange("p (n d) -> p n d", n=HALF),
-                    in_=sat_tokens[b].rearrange("(n p) d -> p n d", p=P)[:, h * HALF : (h + 1) * HALF, :],
+                    out=xs[:].rearrange("p (n d) -> p n d", n=PAIR),
+                    in_=sat_tokens[b].rearrange("(n p) d -> p n d", p=P)[:, h * PAIR : (h + 1) * PAIR, :],
                 )
             st[("xs", unit)] = xs
 
-        def turn_tokens(unit, pair):
-            if pair == 0:
-                st[("grp", unit)] = work.tile([P, HALF * P * 4], BF16, name="grp", tag="grp", align_bytes=64)
-            words_to_groups(
-                st[("xs", unit)][:].bitcast(F32), st[("grp", unit)][:].bitcast(F32), nc.scalar.copy, (pair,)
-            )
+        def turn_tokens(unit):
+            grp = work.tile([P, PAIR * P * 4], BF16, name="grp", tag="grp", bufs=4, align_bytes=64)
+            words_to_groups(st[("xs", unit)][:].bitcast(F32), grp[:].bitcast(F32), nc.scalar.copy)
+            st[("grp", unit)] = grp
 
         def quant_tokens(unit):
-            xc = work.tile([P, HALF * P], U32, name="xc", tag="xc", align_bytes=64)
-            xsc = work.tile([P, HALF * P], U8, name="xsc", tag="xsc", align_bytes=64)
+            xc = work.tile([P, PAIR * P], U32, name="xc", tag="xc", align_bytes=64)
+            xsc = work.tile([P, PAIR * P], U8, name="xsc", tag="xsc", align_bytes=64)
             nc.vector.quantize_mx(out=xc[:].bitcast(FP8X4), scales=xsc[:], in_=st[("grp", unit)][:])
-            ss = small.tile([P, HALF], F32, name="ss", tag="ss")
+            ss = small.tile([P, PAIR], F32, name="ss", tag="ss")
             st[("xc", unit)] = (xc, xsc, ss)
 
         def project(unit, a):
@@ -145,7 +152,7 @@ def tile_sinkhornot_t_kernel(tc, drone_tokens, sat_tokens, Wq, bq, Wk, bk, out_0
                 start=True,
                 stop=True,
             )
-            y = work.tile([P, D], F32, name="y", tag="y", bufs=8)
+            y = work.tile([P, D], F32, name="y", tag="y", bufs=5)
             nc.vector.tensor_tensor(out=y[:], in0=yp[:], in1=bias_b[side][:], op=ALU.add)
             sq = work.tile([P, D], BF16, name="sq", tag="sq", bufs=1)
             nc.scalar.activation(out=sq[:], in_=y[:], func=ACT.Square, accum_out=ss[:, a : a + 1])
@@ -153,12 +160,12 @@ def tile_sinkhornot_t_kernel(tc, drone_tokens, sat_tokens, Wq, bq, Wk, bk, out_0
 
         def normalise(unit):
             ss = st[("xc", unit)][2]
-            ssc = small.tile([P, HALF], F32, name="ssc", tag="ssc")
+            ssc = small.tile([P, PAIR], F32, name="ssc", tag="ssc")
             nc.vector.tensor_scalar_max(out=ssc[:], in0=ss[:], scalar1=1e-24)
-            rn = small.tile([P, HALF], F32, name="rn", tag="rn")
+            rn = small.tile([P, PAIR], F32, name="rn", tag="rn")
             nc.gpsimd.tensor_tensor(out=rn[:], in0=ssc[:], in1=mhalf[:], op=ALU.pow)
-            qh = work.tile([P, HALF * D], BF16, name="qh", tag="qh")
-            for a in range(HALF):
+            qh = work.tile([P, PAIR * D], BF16, name="qh", tag="qh")
+            for a in range(PAIR):
                 nc.vector.tensor_scalar(
                     out=qh[:, a * D : (a + 1) * D],
                     in0=st[("y", unit, a)][:],
@@ -168,21 +175,18 @@ def tile_sinkhornot_t_kernel(tc, drone_tokens, sat_tokens, Wq, bq, Wk, bk, out_0
                 )
             st[("qh", unit)] = qh
 
-        def turn_rows(unit, pair):
-            if pair == 0:
-                st[("qg", unit)] = work.tile([P, HALF * P * 4], BF16, name="grp", tag="grp", align_bytes=64)
-            words_to_groups(
-                st[("qh", unit)][:].bitcast(F32), st[("qg", unit)][:].bitcast(F32), nc.scalar.copy, (pair,)
-            )
+        def turn_rows(unit):
+            qg = work.tile([P, PAIR * P * 4], BF16, name="grp", tag="grp", bufs=4, align_bytes=64)
+            words_to_groups(st[("qh", unit)][:].bitcast(F32), qg[:].bitcast(F32), nc.scalar.copy)
+            st[("qg", unit)] = qg
 
         def quant_rows(unit):
             b, side, h = unit
             if (side, b) not in codes:
                 open_codes(b)
+            cols = slice(h * PAIR * P, (h + 1) * PAIR * P)
             nc.vector.quantize_mx(
-                out=codes[(side, b)][:, h * 512 : (h + 1) * 512].bitcast(FP8X4),
-                scales=scl[(side, b)][:, h * 512 : (h + 1) * 512],
-                in_=st[("qg", unit)][:],
+                out=codes[(side, b)][:, cols].bitcast(FP8X4), scales=scl[(side, b)][:, cols], in_=st[("qg", unit)][:]
             )
 
         def open_codes(b):
@@ -237,12 +241,19 @@ def tile_sinkhornot_t_kernel(tc, drone_tokens, sat_tokens, Wq, bq, Wk, bk, out_0
                 accum_out=st[("r0", b)][:, it, hh : hh + 1],
             )
 
-        def fill_split(b, it):
-            kh, kl = km[b][:2]
-            e = st[("e", b, it)]
+        def fill_hi(b, it):
             cols = slice(it * T, (it + 1) * T)
-            nc.vector.tensor_copy(out=kh[:, cols], in_=e[:])
-            nc.vector.tensor_tensor(out=kl[:, cols], in0=e[:], in1=kh[:, cols], op=ALU.subtract)
+            nc.vector.tensor_copy(out=km[b][0][:, cols], in_=st[("e", b, it)][:])
+
+        def fill_lo(b, it):
+            for hh in range(2):
+                part = slice(it * T + hh * 512, it * T + (hh + 1) * 512)
+                nc.vector.tensor_tensor(
+                    out=km[b][1][:, part],
+                    in0=st[("e", b, it)][:, hh * 512 : (hh + 1) * 512],
+                    in1=km[b][0][:, part],
+                    op=ALU.subtract,
+                )
 
         def fill_turned(b, jt, hh):
             sp = s_turned(b, jt, hh)
@@ -293,8 +304,8 @@ def tile_sinkhornot_t_kernel(tc, drone_tokens, sat_tokens, Wq, bq, Wk, bk, out_0
             v8 = small.tile([P, NT], F32, name="v8", tag="v8", bufs=8)
             new = []
             slot = 0
-            for s in range(2):
-                for o in range(NT):
+            for s, outputs in PASSES:
+                for o in outputs:
                     for c in range(NH):
                         it, jt = (o, s * NH + c) if rows else (s * NH + c, o)
                         for i, k in enumerate(k2):
@@ -339,12 +350,22 @@ def tile_sinkhornot_t_kernel(tc, drone_tokens, sat_tokens, Wq, bq, Wk, bk, out_0
                 out=st[("e", b, it)][:, hh * 512 : (hh + 1) * 512], in_=sp[:], func=ACT.Exp, scale=10.0
             )
 
-        def plan_store(b, it):
+        def plan_product(b, it):
             e = st[("e", b, it)]
             u8 = uv[(b, 0)][0]
-            nc.vector.scalar_tensor_tensor(
-                out=e[:], in0=e[:], scalar=u8[:, it : it + 1], in1=st[("vb", b)][:], op0=ALU.mult, op1=ALU.mult
-            )
+            for hh in range(2):
+                cols = slice(hh * 512, (hh + 1) * 512)
+                nc.vector.scalar_tensor_tensor(
+                    out=e[:, cols],
+                    in0=e[:, cols],
+                    scalar=u8[:, it : it + 1],
+                    in1=st[("vb", b)][:, cols],
+                    op0=ALU.mult,
+                    op1=ALU.mult,
+                )
+
+        def plan_cost(b, it):
+            e = st[("e", b, it)]
             for hh in range(2):
                 junk = work.tile([P, 512], F32, name="junk", tag="junk", bufs=1)
                 col = (b * NT + it) * 2 + hh
@@ -367,86 +388,80 @@ def tile_sinkhornot_t_kernel(tc, drone_tokens, sat_tokens, Wq, bq, Wk, bk, out_0
         plan_at = {}
         last = 0
         for b in range(B):
-            m0 = FIRST_STEP + SPACING * b
-            order = [(b, 1, 0), (b, 1, 1), (b, 0, 0), (b, 0, 1)]
-            for i, unit in enumerate(order):
-                unit_at[i if b == 0 else m0 - 12 + i] = unit
+            m0 = FIRST_STEP + STEPS * b
+            for i in range(2 * UNITS):
+                t = i // 2 if b == 0 else m0 - 18 + i
+                unit_at.setdefault(t, []).append((b, 1 - i // UNITS, i % UNITS))
             for it in range(NT):
-                fill_at.setdefault(m0 - 4 + it // 2, []).append((b, it))
-                turned_at.setdefault(m0 - 3 + it // 2, []).append((b, it))
+                fill_at.setdefault(m0 - 4 + it // 2 if b == 0 else m0 - 8 + it, []).append((b, it))
+                turned_at.setdefault(m0 - 3 + it // 2 if b == 0 else m0 - 5 + it * 6 // NT, []).append((b, it))
+                plan_at.setdefault(m0 + STEPS + 1 + it, []).append((b, it))
             for n in range(STEPS):
-                step_at.setdefault(m0 + n, []).append((b, n))
+                step_at[m0 + n] = (b, n)
             spread_at[m0 + STEPS] = b
-            for it in range(NT):
-                t = m0 + STEPS + 1 + it
-                plan_at.setdefault(t, []).append((b, it))
-                last = max(last, t)
+            last = m0 + STEPS + NT
 
-        for side, w in ((1, Wk), (0, Wq)):
-            weights(side, w)
-        for t in range(2):
-            if t in unit_at:
-                load(unit_at[t])
+        raw_k = load_weights(Wk)
+        for unit in unit_at[0]:
+            load(unit)
+        raw_q = load_weights(Wq)
+        weights(1, raw_k)
+        for unit in unit_at[1]:
+            load(unit)
         for t in range(last + 1):
-            if t + 2 in unit_at:
-                load(unit_at[t + 2])
-            if t - 3 in unit_at:
-                normalise(unit_at[t - 3])
-            mx = [[], []]
+            for unit in unit_at.get(t + 2, []):
+                load(unit)
+            if t == 1:
+                weights(0, raw_q)
+            for unit in unit_at.get(t - 3, []):
+                normalise(unit)
+            mx = []
             for b, it in fill_at.get(t, []):
                 if it == 0:
                     open_k(b)
                 for hh in range(2):
-                    mx[0].append(lambda b=b, it=it, hh=hh: fill_exp(b, it, hh))
+                    mx.append(lambda b=b, it=it, hh=hh: fill_exp(b, it, hh))
+            for unit in unit_at.get(t - 2, []):
+                for a in range(PAIR):
+                    mx.append(lambda u=unit, a=a: project(u, a))
             for b, jt in turned_at.get(t, []):
                 for hh in range(2):
-                    mx[1].append(lambda b=b, jt=jt, hh=hh: fill_turned(b, jt, hh))
-            if t - 2 in unit_at:
-                for a in range(HALF):
-                    mx[a // 2].append(lambda u=unit_at[t - 2], a=a: project(u, a))
+                    mx.append(lambda b=b, jt=jt, hh=hh: fill_turned(b, jt, hh))
             for b, it in plan_at.get(t, []):
                 for hh in range(2):
-                    mx[1].append(lambda b=b, it=it, hh=hh: plan_exp(b, it, hh))
+                    mx.append(lambda b=b, it=it, hh=hh: plan_exp(b, it, hh))
             turns = []
-            for pair in range(2):
-                if t - 4 in unit_at:
-                    turns.append(lambda u=unit_at[t - 4], pair=pair: turn_rows(u, pair))
-            for pair in range(2):
-                if t in unit_at:
-                    turns.append(lambda u=unit_at[t], pair=pair: turn_tokens(u, pair))
+            for unit in unit_at.get(t - 4, []):
+                turns.append(lambda u=unit: turn_rows(u))
+            for unit in unit_at.get(t, []):
+                turns.append(lambda u=unit: turn_tokens(u))
             for b, it in fill_at.get(t - 1, []):
                 turns.append(lambda b=b, it=it: fill_turn(b, it))
             if t in spread_at:
                 turns.append(lambda b=spread_at[t]: spread(b))
-            late = [[], []]
-            if t - 1 in unit_at:
-                late[0].append(lambda u=unit_at[t - 1]: quant_tokens(u))
-            if t - 5 in unit_at:
-                late[0].append(lambda u=unit_at[t - 5]: quant_rows(u))
+            late = []
+            for unit in unit_at.get(t - 1, []):
+                late.append(lambda u=unit: quant_tokens(u))
+            for unit in unit_at.get(t - 5, []):
+                late.append(lambda u=unit: quant_rows(u))
             for b, it in fill_at.get(t, []):
-                late[0].append(lambda b=b, it=it: fill_split(b, it))
+                late.append(lambda b=b, it=it: fill_hi(b, it))
             for b, it in plan_at.get(t, []):
-                late[1].append(lambda b=b, it=it: plan_store(b, it))
-            steps = step_at.get(t, [])
-            mx = mx[0] + mx[1]
-            late = late[0] + late[1]
-            if steps:
-                apart = len(turns) // 4 * 2
-                while len(mx) < apart + 5:
+                late.append(lambda b=b, it=it: plan_product(b, it))
+            for b, it in fill_at.get(t, []):
+                late.append(lambda b=b, it=it: fill_lo(b, it))
+            for b, it in plan_at.get(t, []):
+                late.append(lambda b=b, it=it: plan_cost(b, it))
+            if t in step_at:
+                while len(mx) < WIDE:
                     mx.append(spare)
-                for i in range(2):
-                    (mx.pop(0) if len(mx) > apart + 5 else spare)()
-                half_step(steps[0][0], steps[0][1], mx[: len(mx) - apart])
-                rest = mx[len(mx) - apart :]
-                for i, call in enumerate(turns):
-                    call()
-                    if i % 4 == 1 and rest:
-                        rest.pop(0)()
-                        rest.pop(0)()
+                for i in range(KICK):
+                    mx.pop(0)()
+                half_step(step_at[t][0], step_at[t][1], mx)
             else:
-                for call in mx + turns:
+                for call in mx:
                     call()
-            for call in late:
+            for call in turns + late:
                 call()
 
         tp = psum.tile([P, B * NT * 2], F32, name="tp", tag="mm", bufs=8)

@@ -24,7 +24,7 @@ COLS = 4
 PASSES = ((0, (0, 1, 2, 3, 4, 5)), (1, (0, 1, 2, 3)), (0, (6, 7)), (1, (4, 5, 6, 7)))
 ITERS = 5
 STEPS = 2 * ITERS - 1
-FIRST_STEP = 12
+FIRST_STEP = 11
 WIDE = 7
 KICK = 2
 
@@ -154,7 +154,7 @@ def tile_sinkhornot_t_kernel(tc, drone_tokens, sat_tokens, Wq, bq, Wk, bk, out_0
             )
             y = work.tile([P, D], F32, name="y", tag="y", bufs=5)
             nc.vector.tensor_tensor(out=y[:], in0=yp[:], in1=bias_b[side][:], op=ALU.add)
-            sq = work.tile([P, D], BF16, name="sq", tag="sq", bufs=1)
+            sq = work.tile([P, D], BF16, name="sq", tag="sq", bufs=2)
             nc.scalar.activation(out=sq[:], in_=y[:], func=ACT.Square, accum_out=ss[:, a : a + 1])
             st[("y", unit, a)] = y
 
@@ -390,11 +390,11 @@ def tile_sinkhornot_t_kernel(tc, drone_tokens, sat_tokens, Wq, bq, Wk, bk, out_0
         for b in range(B):
             m0 = FIRST_STEP + STEPS * b
             for i in range(2 * UNITS):
-                t = i // 2 if b == 0 else m0 - 18 + i
+                t = i // 2 if b == 0 else m0 - 18 + i + (b == 1)
                 unit_at.setdefault(t, []).append((b, 1 - i // UNITS, i % UNITS))
             for it in range(NT):
                 fill_at.setdefault(m0 - 4 + it // 2 if b == 0 else m0 - 8 + it, []).append((b, it))
-                turned_at.setdefault(m0 - 3 + it // 2 if b == 0 else m0 - 5 + it * 6 // NT, []).append((b, it))
+                turned_at.setdefault(m0 - 3 + it // 2 if b == 0 else m0 - 4 + it * 5 // NT, []).append((b, it))
                 plan_at.setdefault(m0 + STEPS + 1 + it, []).append((b, it))
             for n in range(STEPS):
                 step_at[m0 + n] = (b, n)
@@ -440,9 +440,9 @@ def tile_sinkhornot_t_kernel(tc, drone_tokens, sat_tokens, Wq, bq, Wk, bk, out_0
             if t in spread_at:
                 turns.append(lambda b=spread_at[t]: spread(b))
             late = []
-            for unit in unit_at.get(t - 1, []):
+            for unit in unit_at.get(t, []):
                 late.append(lambda u=unit: quant_tokens(u))
-            for unit in unit_at.get(t - 5, []):
+            for unit in unit_at.get(t - 4, []):
                 late.append(lambda u=unit: quant_rows(u))
             for b, it in fill_at.get(t, []):
                 late.append(lambda b=b, it=it: fill_hi(b, it))

@@ -21,6 +21,8 @@ PAIR = 2
 UNITS = NT // PAIR
 NH = NT // 2
 COLS = 4
+TAIL_FIRST = 2
+TAIL_COL = (B - 1) * NT * 2
 PASSES = ((0, (0, 1, 2, 3, 4, 5)), (1, (0, 1, 2, 3)), (0, (6, 7)), (1, (4, 5, 6, 7)))
 ITERS = 5
 STEPS = 2 * ITERS - 1
@@ -55,7 +57,7 @@ def tile_sinkhornot_t_kernel(tc, drone_tokens, sat_tokens, Wq, bq, Wk, bk, out_0
         nc.vector.memset(ones_f[:], 1.0)
         mhalf = keep.tile([P, PAIR], F32, name="mhalf")
         nc.vector.memset(mhalf[:], -0.5)
-        ota = keep.tile([P, B * NT * 2], F32, name="ota")
+        ota = keep.tile([P, TAIL_COL + 1], F32, name="ota")
         first = small.tile([P, 1], F32, name="first", tag="first", bufs=1)
         nc.scalar.activation(out=first[:], in_=ones_f[:, 0:1], func=ACT.Exp)
         vps_all = []
@@ -350,6 +352,69 @@ def tile_sinkhornot_t_kernel(tc, drone_tokens, sat_tokens, Wq, bq, Wk, bk, out_0
                 out=st[("e", b, it)][:, hh * 512 : (hh + 1) * 512], in_=sp[:], func=ACT.Exp, scale=10.0
             )
 
+        def open_tail(b):
+            parts = []
+            for part in ("kh", "kl", "kth", "ktl"):
+                kt = kpool.tile([P, NT * T], BF16, name=part)
+                parts.append(kt[:].bitcast(F32))
+            for it in range(NT):
+                cols = slice(it % NH * T, (it % NH + 1) * T)
+                st[("w", b, it)] = parts[it // NH][:, cols]
+                st[("e", b, it)] = parts[2 + it // NH][:, cols]
+
+        def tail_exp(b, it, hh):
+            cols = slice(hh * 512, (hh + 1) * 512)
+            sp = s_pass(b, it, hh, "mm")
+            nc.scalar.activation(out=st[("e", b, it)][:, cols], in_=sp[:], func=ACT.Exp, scale=10.0)
+            nc.vector.scalar_tensor_tensor(
+                out=st[("w", b, it)][:, cols],
+                in0=sp[:],
+                scalar=1.0,
+                in1=st[("e", b, it)][:, cols],
+                op0=ALU.subtract,
+                op1=ALU.mult,
+            )
+
+        def tail_turn(b, it):
+            if it == 0:
+                cts = []
+                for h in range(2):
+                    ct = psum.tile([P, 512], F32, name="ct", tag="mm", bufs=8)
+                    cts.append(ct)
+                st["ct"] = cts
+            u8 = uv[(b, 0)][0]
+            yk = work.tile([P, T], F32, name="yk", tag="e", bufs=3)
+            nc.scalar.activation(out=yk[:], in_=st[("w", b, it)], func=ACT.Copy, scale=u8[:, it : it + 1])
+            for jt in range(NT):
+                nc.tensor.matmul(
+                    out=st["ct"][jt // 4][:, jt % 4 * P : (jt % 4 + 1) * P],
+                    lhsT=yk[:, jt * P : (jt + 1) * P],
+                    rhs=ident_f[:],
+                    is_transpose=True,
+                    start=(it == 0 and jt % 4 == 0),
+                    stop=(it == NT - 1 and jt % 4 == 3),
+                )
+
+        def tail_sum(b):
+            c8 = small.tile([P, NT], F32, name="c8", tag="c8", bufs=1)
+            for h in range(2):
+                nc.vector.tensor_reduce(
+                    out=c8[:, h * NH : (h + 1) * NH],
+                    in_=st["ct"][h][:].rearrange("p (q m) -> p q m", m=P),
+                    axis=AX.X,
+                    op=ALU.add,
+                )
+            cv = small.tile([P, NT], F32, name="cv", tag="cv", bufs=1)
+            nc.vector.scalar_tensor_tensor(
+                out=cv[:],
+                in0=c8[:],
+                scalar=1.0,
+                in1=uv[(b, 1)][0][:],
+                op0=ALU.mult,
+                op1=ALU.mult,
+                accum_out=ota[:, TAIL_COL : TAIL_COL + 1],
+            )
+
         def plan_product(b, it):
             e = st[("e", b, it)]
             u8 = uv[(b, 0)][0]
@@ -366,7 +431,7 @@ def tile_sinkhornot_t_kernel(tc, drone_tokens, sat_tokens, Wq, bq, Wk, bk, out_0
 
         def plan_cost(b, it):
             e = st[("e", b, it)]
-            for hh in range(2):
+            for hh in range(2 if b < B - 1 else 0):
                 junk = work.tile([P, 512], F32, name="junk", tag="junk", bufs=1)
                 col = (b * NT + it) * 2 + hh
                 nc.vector.scalar_tensor_tensor(
@@ -386,6 +451,7 @@ def tile_sinkhornot_t_kernel(tc, drone_tokens, sat_tokens, Wq, bq, Wk, bk, out_0
         step_at = {}
         spread_at = {}
         plan_at = {}
+        tail_at = {}
         last = 0
         for b in range(B):
             m0 = FIRST_STEP + STEPS * b
@@ -398,6 +464,9 @@ def tile_sinkhornot_t_kernel(tc, drone_tokens, sat_tokens, Wq, bq, Wk, bk, out_0
                 plan_at.setdefault(m0 + STEPS + 1 + it, []).append((b, it))
             for n in range(STEPS):
                 step_at[m0 + n] = (b, n)
+            if b == B - 1:
+                for it in range(NT):
+                    tail_at[m0 + 0 + it] = [(b, it)]
             spread_at[m0 + STEPS] = b
             last = m0 + STEPS + NT
 
@@ -428,18 +497,31 @@ def tile_sinkhornot_t_kernel(tc, drone_tokens, sat_tokens, Wq, bq, Wk, bk, out_0
                 for hh in range(2):
                     mx.append(lambda b=b, jt=jt, hh=hh: fill_turned(b, jt, hh))
             for b, it in plan_at.get(t, []):
+                if b < B - 1:
+                    for hh in range(2):
+                        mx.append(lambda b=b, it=it, hh=hh: plan_exp(b, it, hh))
+            for b, it in tail_at.get(t, []):
+                if it == 0:
+                    open_tail(b)
                 for hh in range(2):
-                    mx.append(lambda b=b, it=it, hh=hh: plan_exp(b, it, hh))
+                    mx.append(lambda b=b, it=it, hh=hh: tail_exp(b, it, hh))
             turns = []
+            late = []
             for unit in unit_at.get(t - 4, []):
                 turns.append(lambda u=unit: turn_rows(u))
             for unit in unit_at.get(t, []):
                 turns.append(lambda u=unit: turn_tokens(u))
             for b, it in fill_at.get(t - 1, []):
                 turns.append(lambda b=b, it=it: fill_turn(b, it))
+            if t + 1 in spread_at and spread_at[t + 1] == B - 1:
+                for it in range(TAIL_FIRST):
+                    turns.append(lambda it=it: tail_turn(B - 1, it))
             if t in spread_at:
                 turns.append(lambda b=spread_at[t]: spread(b))
-            late = []
+                if spread_at[t] == B - 1:
+                    for it in range(TAIL_FIRST, NT):
+                        turns.append(lambda it=it: tail_turn(B - 1, it))
+                    late.append(lambda: tail_sum(B - 1))
             for unit in unit_at.get(t, []):
                 late.append(lambda u=unit: quant_tokens(u))
             for unit in unit_at.get(t - 4, []):
@@ -464,7 +546,7 @@ def tile_sinkhornot_t_kernel(tc, drone_tokens, sat_tokens, Wq, bq, Wk, bk, out_0
             for call in turns + late:
                 call()
 
-        tp = psum.tile([P, B * NT * 2], F32, name="tp", tag="mm", bufs=8)
+        tp = psum.tile([P, TAIL_COL + 1], F32, name="tp", tag="mm", bufs=8)
         nc.tensor.matmul(out=tp[:], lhsT=ones_f[:], rhs=ota[:], start=True, stop=True)
         tot = small.tile([P, 1], F32, name="tot", tag="tot")
         nc.vector.tensor_reduce(out=tot[:], in_=tp[:], axis=AX.X, op=ALU.add)

@@ -20,14 +20,14 @@ NT = T // P
 PAIR = 2
 UNITS = NT // PAIR
 NH = NT // 2
-COLS = 4
+COLS = 5
 TAIL_FIRST = 2
 TAIL_COL = (B - 1) * NT * 2
 PASSES = ((0, (0, 1, 2, 3, 4, 5)), (1, (0, 1, 2, 3)), (0, (6, 7)), (1, (4, 5, 6, 7)))
 ITERS = 5
 STEPS = 2 * ITERS - 1
 FIRST_STEP = 11
-WIDE = 7
+WIDE = 6
 KICK = 2
 
 FLOPS = 2 * 2 * B * T * D * D + 2 * B * T * T * D

from contextlib import ExitStack

import concourse.mybir as mybir
from concourse.masks import make_identity

F32 = mybir.dt.float32
BF16 = mybir.dt.bfloat16
U32 = mybir.dt.uint32
U8 = mybir.dt.uint8
FP8X4 = mybir.dt.float8_e4m3fn_x4
ACT = mybir.ActivationFunctionType
ALU = mybir.AluOpType
AX = mybir.AxisListType

P = 128
B = 4
T = 1024
D = 512
NT = T // P
PAIR = 2
UNITS = NT // PAIR
NH = NT // 2
COLS = 5
TAIL_FIRST = 2
TAIL_COL = (B - 1) * NT * 2
PASSES = ((0, (0, 1, 2, 3, 4, 5)), (1, (0, 1, 2, 3)), (0, (6, 7)), (1, (4, 5, 6, 7)))
ITERS = 5
STEPS = 2 * ITERS - 1
FIRST_STEP = 11
WIDE = 6
KICK = 2

FLOPS = 2 * 2 * B * T * D * D + 2 * B * T * T * D


def tile_sinkhornot_t_kernel(tc, drone_tokens, sat_tokens, Wq, bq, Wk, bk, out_0, out_1):
    nc = tc.nc
    with ExitStack() as ctx:
        ctx.enter_context(tc.manual_schedule(engines={mybir.EngineType.PE, mybir.EngineType.SP}))
        keep = ctx.enter_context(tc.tile_pool(name="keep", bufs=1))
        small = ctx.enter_context(tc.tile_pool(name="small", bufs=4))
        kpool = ctx.enter_context(tc.tile_pool(name="kpool", bufs=2))
        cpool = ctx.enter_context(tc.tile_pool(name="cpool", bufs=4))
        work = ctx.enter_context(tc.tile_pool(name="work", bufs=2))
        psum = ctx.enter_context(tc.psum_pool(name="psum", bufs=2))

        bias_b = []
        for side, bvec in enumerate((bq, bk)):
            bt = keep.tile([P, D], BF16, name="bias%d" % side)
            nc.scalar.dma_start(out=bt[:], in_=bvec.partition_broadcast(P))
            bias_b.append(bt)
        ident_f = keep.tile([P, P], F32, name="ident_f")
        make_identity(nc, ident_f[:])
        ident_b = keep.tile([P, P], BF16, name="ident_b")
        make_identity(nc, ident_b[:])
        ones_f = keep.tile([P, P], F32, name="ones_f")
        nc.vector.memset(ones_f[:], 1.0)
        mhalf = keep.tile([P, PAIR], F32, name="mhalf")
        nc.vector.memset(mhalf[:], -0.5)
        ota = keep.tile([P, TAIL_COL + 1], F32, name="ota")
        first = small.tile([P, 1], F32, name="first", tag="first", bufs=1)
        nc.scalar.activation(out=first[:], in_=ones_f[:, 0:1], func=ACT.Exp)
        vps_all = []
        for i in range(8):
            vp = keep.tile([P, NH, COLS], BF16, name="vp%d" % i)
            nc.vector.memset(vp[:], 0.0)
            vps_all.append(vp)

        wcodes = [keep.tile([P, D], U32, name="wc%d" % s, align_bytes=64) for s in range(2)]
        wscl = [keep.tile([P, D], U8, name="ws%d" % s, align_bytes=64) for s in range(2)]
        codes = {}
        scl = {}

        def words_to_groups(src_f, grp_f, copy):
            xt = psum.tile([P, 512], F32, name="xt", tag="mm", bufs=8)
            for a in range(PAIR):
                for u in range(2):
                    nc.tensor.transpose(
                        out=xt[:, (a * 2 + u) * P : (a * 2 + u + 1) * P],
                        in_=src_f[:, a * 256 + u * P : a * 256 + (u + 1) * P],
                        identity=ident_f[:],
                    )
            copy(
                out=grp_f.rearrange("p (a r u) -> p a r u", a=PAIR, u=2),
                in_=xt[:].rearrange("p (a u r) -> p a r u", a=PAIR, u=2),
            )

        def spare():
            sp = psum.tile([P, D], F32, name="spare", tag="mm", bufs=8)
            nc.tensor.matmul_mx(
                out=sp[:],
                lhsT=wcodes[0][:, 0:P].bitcast(FP8X4),
                lhsT_scale=wscl[0][:, 0:P],
                rhs=wcodes[1][:].bitcast(FP8X4),
                rhs_scale=wscl[1][:],
                start=True,
                stop=True,
            )

        def load_weights(w):
            raw = work.tile([P, 4 * D], BF16, name="raw", tag="raw", bufs=2)
            nc.sync.dma_start(
                out=raw[:].rearrange("p (n d) -> p n d", n=4), in_=w.rearrange("(n p) d -> p n d", p=P)
            )
            return raw

        def weights(side, raw):
            words = raw[:].bitcast(F32)
            for i in range(2):
                grp = work.tile([P, PAIR * P * 4], BF16, name="grp", tag="grp", bufs=4, align_bytes=64)
                words_to_groups(words[:, i * 512 : (i + 1) * 512], grp[:].bitcast(F32), nc.vector.tensor_copy)
                cols = slice(i * PAIR * P, (i + 1) * PAIR * P)
                nc.vector.quantize_mx(out=wcodes[side][:, cols].bitcast(FP8X4), scales=wscl[side][:, cols], in_=grp[:])

        st = {}

        def load(unit):
            b, side, h = unit
            xs = work.tile([P, PAIR * D], BF16, name="xs", tag="xs", bufs=4)
            if side == 0:
                nc.sync.dma_start(
                    out=xs[:],
                    in_=drone_tokens[b].rearrange("(p n) d -> p (n d)", n=NT)[:, h * PAIR * D : (h + 1) * PAIR * D],
                )
            else:
                nc.sync.dma_start(
                    out=xs[:].rearrange("p (n d) -> p n d", n=PAIR),
                    in_=sat_tokens[b].rearrange("(n p) d -> p n d", p=P)[:, h * PAIR : (h + 1) * PAIR, :],
                )
            st[("xs", unit)] = xs

        def turn_tokens(unit):
            grp = work.tile([P, PAIR * P * 4], BF16, name="grp", tag="grp", bufs=4, align_bytes=64)
            words_to_groups(st[("xs", unit)][:].bitcast(F32), grp[:].bitcast(F32), nc.scalar.copy)
            st[("grp", unit)] = grp

        def quant_tokens(unit):
            xc = work.tile([P, PAIR * P], U32, name="xc", tag="xc", align_bytes=64)
            xsc = work.tile([P, PAIR * P], U8, name="xsc", tag="xsc", align_bytes=64)
            nc.vector.quantize_mx(out=xc[:].bitcast(FP8X4), scales=xsc[:], in_=st[("grp", unit)][:])
            ss = small.tile([P, PAIR], F32, name="ss", tag="ss")
            st[("xc", unit)] = (xc, xsc, ss)

        def project(unit, a):
            side = unit[1]
            xc, xsc, ss = st[("xc", unit)]
            yp = psum.tile([P, D], F32, name="yp", tag="mm", bufs=8)
            nc.tensor.matmul_mx(
                out=yp[:],
                lhsT=xc[:, a * P : (a + 1) * P].bitcast(FP8X4),
                lhsT_scale=xsc[:, a * P : (a + 1) * P],
                rhs=wcodes[side][:].bitcast(FP8X4),
                rhs_scale=wscl[side][:],
                start=True,
                stop=True,
            )
            y = work.tile([P, D], F32, name="y", tag="y", bufs=5)
            nc.vector.tensor_tensor(out=y[:], in0=yp[:], in1=bias_b[side][:], op=ALU.add)
            sq = work.tile([P, D], BF16, name="sq", tag="sq", bufs=2)
            nc.scalar.activation(out=sq[:], in_=y[:], func=ACT.Square, accum_out=ss[:, a : a + 1])
            st[("y", unit, a)] = y

        def normalise(unit):
            ss = st[("xc", unit)][2]
            ssc = small.tile([P, PAIR], F32, name="ssc", tag="ssc")
            nc.vector.tensor_scalar_max(out=ssc[:], in0=ss[:], scalar1=1e-24)
            rn = small.tile([P, PAIR], F32, name="rn", tag="rn")
            nc.gpsimd.tensor_tensor(out=rn[:], in0=ssc[:], in1=mhalf[:], op=ALU.pow)
            qh = work.tile([P, PAIR * D], BF16, name="qh", tag="qh")
            for a in range(PAIR):
                nc.vector.tensor_scalar(
                    out=qh[:, a * D : (a + 1) * D],
                    in0=st[("y", unit, a)][:],
                    scalar1=rn[:, a : a + 1],
                    scalar2=None,
                    op0=ALU.mult,
                )
            st[("qh", unit)] = qh

        def turn_rows(unit):
            qg = work.tile([P, PAIR * P * 4], BF16, name="grp", tag="grp", bufs=4, align_bytes=64)
            words_to_groups(st[("qh", unit)][:].bitcast(F32), qg[:].bitcast(F32), nc.scalar.copy)
            st[("qg", unit)] = qg

        def quant_rows(unit):
            b, side, h = unit
            if (side, b) not in codes:
                open_codes(b)
            cols = slice(h * PAIR * P, (h + 1) * PAIR * P)
            nc.vector.quantize_mx(
                out=codes[(side, b)][:, cols].bitcast(FP8X4), scales=scl[(side, b)][:, cols], in_=st[("qg", unit)][:]
            )

        def open_codes(b):
            for side in range(2):
                codes[(side, b)] = cpool.tile([P, T], U32, name="c%d" % side, align_bytes=64)
                scl[(side, b)] = cpool.tile([P, T], U8, name="s%d" % side, align_bytes=64)

        def s_turned(b, jt, hh):
            sp = psum.tile([P, 512], F32, name="sp", tag="mm", bufs=8)
            nc.tensor.matmul_mx(
                out=sp[:],
                lhsT=codes[(1, b)][:, jt * P : (jt + 1) * P].bitcast(FP8X4),
                lhsT_scale=scl[(1, b)][:, jt * P : (jt + 1) * P],
                rhs=codes[(0, b)][:, hh * 512 : (hh + 1) * 512].bitcast(FP8X4),
                rhs_scale=scl[(0, b)][:, hh * 512 : (hh + 1) * 512],
                start=True,
                stop=True,
            )
            return sp

        def s_pass(b, it, hh, tag):
            sp = psum.tile([P, 512], F32, name="sp", tag="mm", bufs=8)
            nc.tensor.matmul_mx(
                out=sp[:],
                lhsT=codes[(0, b)][:, it * P : (it + 1) * P].bitcast(FP8X4),
                lhsT_scale=scl[(0, b)][:, it * P : (it + 1) * P],
                rhs=codes[(1, b)][:, hh * 512 : (hh + 1) * 512].bitcast(FP8X4),
                rhs_scale=scl[(1, b)][:, hh * 512 : (hh + 1) * 512],
                start=True,
                stop=True,
            )
            return sp

        km = {}

        def open_k(b):
            km[b] = []
            for part in ("kh", "kl", "kth", "ktl"):
                kt = kpool.tile([P, NT * T], BF16, name=part)
                km[b].append(kt)
            st[("r0", b)] = small.tile([P, NT, 2], F32, name="r0", tag="r0")

        def fill_exp(b, it, hh):
            if hh == 0:
                st[("e", b, it)] = work.tile([P, T], F32, name="e", tag="e", bufs=3)
            sp = s_pass(b, it, hh, "mm")
            nc.scalar.activation(
                out=st[("e", b, it)][:, hh * 512 : (hh + 1) * 512],
                in_=sp[:],
                func=ACT.Exp,
                scale=10.0,
                accum_out=st[("r0", b)][:, it, hh : hh + 1],
            )

        def fill_hi(b, it):
            cols = slice(it * T, (it + 1) * T)
            nc.vector.tensor_copy(out=km[b][0][:, cols], in_=st[("e", b, it)][:])

        def fill_lo(b, it):
            for hh in range(2):
                part = slice(it * T + hh * 512, it * T + (hh + 1) * 512)
                nc.vector.tensor_tensor(
                    out=km[b][1][:, part],
                    in0=st[("e", b, it)][:, hh * 512 : (hh + 1) * 512],
                    in1=km[b][0][:, part],
                    op=ALU.subtract,
                )

        def fill_turned(b, jt, hh):
            sp = s_turned(b, jt, hh)
            lo = jt * T + hh * 512
            nc.scalar.activation(out=km[b][2][:, lo : lo + 512], in_=sp[:], func=ACT.Exp, scale=10.0)

        def fill_turn(b, it):
            k, kt = km[b][1], km[b][3]
            tb = psum.tile([P, T], BF16, name="tb", tag="mm", bufs=8)
            for jt in range(NT):
                nc.tensor.transpose(
                    out=tb[:, jt * P : (jt + 1) * P],
                    in_=k[:, it * T + jt * P : it * T + (jt + 1) * P],
                    identity=ident_b[:],
                )
            nc.scalar.copy(out=kt[:, it * T : (it + 1) * T], in_=tb[:])

        def inverse(sums, v8, h):
            c4 = small.tile([P, NH], F32, name="c4", tag="c4", bufs=4)
            nc.vector.tensor_reduce(out=c4[:], in_=sums, axis=AX.X, op=ALU.add)
            vp = vps_all[turn[0] % len(vps_all)]
            turn[0] += 1
            with nc.allow_low_precision(reason="the second part carries what this rounding leaves"):
                nc.vector.reciprocal(out=vp[:, :, 0], in_=c4[:])
            cols = slice(h * NH, (h + 1) * NH)
            nc.vector.reciprocal(out=v8[:, cols], in_=c4[:])
            nc.vector.tensor_tensor(out=vp[:, :, 1], in0=v8[:, cols], in1=vp[:, :, 0], op=ALU.subtract)
            return vp

        uv = {}
        turn = [0]

        def half_step(b, n, between):
            if n == 0:
                u8 = small.tile([P, NT], F32, name="v8", tag="v8", bufs=8)
                r0 = st[("r0", b)]
                ups = []
                for h in range(2):
                    ups.append(inverse(r0[:, h * NH : (h + 1) * NH, :], u8, h))
                uv[(b, 0)] = (u8, ups)
            rows = n % 2 == 1
            k2 = km[b][2:] if rows else km[b][:2]
            vps = uv[(b, 1 if rows else 0)][1]
            mvs = []
            for h in range(2):
                mv = psum.tile([P, NH, 2, COLS], F32, name="mv", tag="mm", bufs=8)
                mvs.append(mv)
            v8 = small.tile([P, NT], F32, name="v8", tag="v8", bufs=8)
            new = []
            slot = 0
            for s, outputs in PASSES:
                for o in outputs:
                    for c in range(NH):
                        it, jt = (o, s * NH + c) if rows else (s * NH + c, o)
                        for i, k in enumerate(k2):
                            lo = jt * T + it * P if rows and i == 0 else it * T + jt * P
                            nc.tensor.matmul(
                                out=mvs[o // NH][:, o % NH, s, :],
                                lhsT=k[:, lo : lo + P],
                                rhs=vps[s][:, c, :],
                                start=(c == 0 and i == 0),
                                stop=(c == NH - 1 and i == 1),
                            )
                    for call in between[slot * len(between) // 16 : (slot + 1) * len(between) // 16]:
                        call()
                    slot += 1
                    if s == 1 and o % NH == NH - 1:
                        h = o // NH
                        new.append(inverse(mvs[h][:].rearrange("p o s n -> p o (s n)"), v8, h))
            uv[(b, 0 if rows else 1)] = (v8, new)

        def spread(b):
            v8 = uv[(b, 1)][0]
            vb = work.tile([P, T], F32, name="vb", tag="vb", bufs=1)
            for hh in range(2):
                vbp = psum.tile([P, 512], F32, name="vbp", tag="mm", bufs=8)
                for j in range(4):
                    jt = hh * 4 + j
                    nc.tensor.transpose(
                        out=vbp[:, j * P : (j + 1) * P],
                        in_=v8[:, jt : jt + 1].to_broadcast([P, P]),
                        identity=ident_f[:],
                    )
                nc.scalar.copy(out=vb[:, hh * 512 : (hh + 1) * 512], in_=vbp[:])
            st[("vb", b)] = vb

        def plan_exp(b, it, hh):
            if hh == 0:
                st[("e", b, it)] = work.tile([P, T], F32, name="e", tag="e", bufs=3)
                st[("sp", b, it)] = []
            sp = s_pass(b, it, hh, "tr" if b == B - 1 and it % 2 else "mm")
            st[("sp", b, it)].append(sp)
            nc.scalar.activation(
                out=st[("e", b, it)][:, hh * 512 : (hh + 1) * 512], in_=sp[:], func=ACT.Exp, scale=10.0
            )

        def open_tail(b):
            parts = []
            for part in ("kh", "kl", "kth", "ktl"):
                kt = kpool.tile([P, NT * T], BF16, name=part)
                parts.append(kt[:].bitcast(F32))
            for it in range(NT):
                cols = slice(it % NH * T, (it % NH + 1) * T)
                st[("w", b, it)] = parts[it // NH][:, cols]
                st[("e", b, it)] = parts[2 + it // NH][:, cols]

        def tail_exp(b, it, hh):
            cols = slice(hh * 512, (hh + 1) * 512)
            sp = s_pass(b, it, hh, "mm")
            nc.scalar.activation(out=st[("e", b, it)][:, cols], in_=sp[:], func=ACT.Exp, scale=10.0)
            nc.vector.scalar_tensor_tensor(
                out=st[("w", b, it)][:, cols],
                in0=sp[:],
                scalar=1.0,
                in1=st[("e", b, it)][:, cols],
                op0=ALU.subtract,
                op1=ALU.mult,
            )

        def tail_turn(b, it):
            if it == 0:
                cts = []
                for h in range(2):
                    ct = psum.tile([P, 512], F32, name="ct", tag="mm", bufs=8)
                    cts.append(ct)
                st["ct"] = cts
            u8 = uv[(b, 0)][0]
            yk = work.tile([P, T], F32, name="yk", tag="e", bufs=3)
            nc.scalar.activation(out=yk[:], in_=st[("w", b, it)], func=ACT.Copy, scale=u8[:, it : it + 1])
            for jt in range(NT):
                nc.tensor.matmul(
                    out=st["ct"][jt // 4][:, jt % 4 * P : (jt % 4 + 1) * P],
                    lhsT=yk[:, jt * P : (jt + 1) * P],
                    rhs=ident_f[:],
                    is_transpose=True,
                    start=(it == 0 and jt % 4 == 0),
                    stop=(it == NT - 1 and jt % 4 == 3),
                )

        def tail_sum(b):
            c8 = small.tile([P, NT], F32, name="c8", tag="c8", bufs=1)
            for h in range(2):
                nc.vector.tensor_reduce(
                    out=c8[:, h * NH : (h + 1) * NH],
                    in_=st["ct"][h][:].rearrange("p (q m) -> p q m", m=P),
                    axis=AX.X,
                    op=ALU.add,
                )
            cv = small.tile([P, NT], F32, name="cv", tag="cv", bufs=1)
            nc.vector.scalar_tensor_tensor(
                out=cv[:],
                in0=c8[:],
                scalar=1.0,
                in1=uv[(b, 1)][0][:],
                op0=ALU.mult,
                op1=ALU.mult,
                accum_out=ota[:, TAIL_COL : TAIL_COL + 1],
            )

        def plan_product(b, it):
            e = st[("e", b, it)]
            u8 = uv[(b, 0)][0]
            for hh in range(2):
                cols = slice(hh * 512, (hh + 1) * 512)
                nc.vector.scalar_tensor_tensor(
                    out=e[:, cols],
                    in0=e[:, cols],
                    scalar=u8[:, it : it + 1],
                    in1=st[("vb", b)][:, cols],
                    op0=ALU.mult,
                    op1=ALU.mult,
                )

        def plan_cost(b, it):
            e = st[("e", b, it)]
            for hh in range(2 if b < B - 1 else 0):
                junk = work.tile([P, 512], F32, name="junk", tag="junk", bufs=1)
                col = (b * NT + it) * 2 + hh
                nc.vector.scalar_tensor_tensor(
                    out=junk[:],
                    in0=st[("sp", b, it)][hh][:],
                    scalar=1.0,
                    in1=e[:, hh * 512 : (hh + 1) * 512],
                    op0=ALU.subtract,
                    op1=ALU.mult,
                    accum_out=ota[:, col : col + 1],
                )
            nc.sync.dma_start(out=out_0[b].rearrange("(p n) j -> p n j", n=NT)[:, it, :], in_=e[:])

        unit_at = {}
        fill_at = {}
        turned_at = {}
        step_at = {}
        spread_at = {}
        plan_at = {}
        tail_at = {}
        last = 0
        for b in range(B):
            m0 = FIRST_STEP + STEPS * b
            for i in range(2 * UNITS):
                t = i // 2 if b == 0 else m0 - 18 + i + (b == 1)
                unit_at.setdefault(t, []).append((b, 1 - i // UNITS, i % UNITS))
            for it in range(NT):
                fill_at.setdefault(m0 - 4 + it // 2 if b == 0 else m0 - 8 + it, []).append((b, it))
                turned_at.setdefault(m0 - 3 + it // 2 if b == 0 else m0 - 4 + it * 5 // NT, []).append((b, it))
                plan_at.setdefault(m0 + STEPS + 1 + it, []).append((b, it))
            for n in range(STEPS):
                step_at[m0 + n] = (b, n)
            if b == B - 1:
                for it in range(NT):
                    tail_at[m0 + 0 + it] = [(b, it)]
            spread_at[m0 + STEPS] = b
            last = m0 + STEPS + NT

        raw_k = load_weights(Wk)
        for unit in unit_at[0]:
            load(unit)
        raw_q = load_weights(Wq)
        weights(1, raw_k)
        for unit in unit_at[1]:
            load(unit)
        for t in range(last + 1):
            for unit in unit_at.get(t + 2, []):
                load(unit)
            if t == 1:
                weights(0, raw_q)
            for unit in unit_at.get(t - 3, []):
                normalise(unit)
            mx = []
            for b, it in fill_at.get(t, []):
                if it == 0:
                    open_k(b)
                for hh in range(2):
                    mx.append(lambda b=b, it=it, hh=hh: fill_exp(b, it, hh))
            for unit in unit_at.get(t - 2, []):
                for a in range(PAIR):
                    mx.append(lambda u=unit, a=a: project(u, a))
            for b, jt in turned_at.get(t, []):
                for hh in range(2):
                    mx.append(lambda b=b, jt=jt, hh=hh: fill_turned(b, jt, hh))
            for b, it in plan_at.get(t, []):
                if b < B - 1:
                    for hh in range(2):
                        mx.append(lambda b=b, it=it, hh=hh: plan_exp(b, it, hh))
            for b, it in tail_at.get(t, []):
                if it == 0:
                    open_tail(b)
                for hh in range(2):
                    mx.append(lambda b=b, it=it, hh=hh: tail_exp(b, it, hh))
            turns = []
            late = []
            for unit in unit_at.get(t - 4, []):
                turns.append(lambda u=unit: turn_rows(u))
            for unit in unit_at.get(t, []):
                turns.append(lambda u=unit: turn_tokens(u))
            for b, it in fill_at.get(t - 1, []):
                turns.append(lambda b=b, it=it: fill_turn(b, it))
            if t + 1 in spread_at and spread_at[t + 1] == B - 1:
                for it in range(TAIL_FIRST):
                    turns.append(lambda it=it: tail_turn(B - 1, it))
            if t in spread_at:
                turns.append(lambda b=spread_at[t]: spread(b))
                if spread_at[t] == B - 1:
                    for it in range(TAIL_FIRST, NT):
                        turns.append(lambda it=it: tail_turn(B - 1, it))
                    late.append(lambda: tail_sum(B - 1))
            for unit in unit_at.get(t, []):
                late.append(lambda u=unit: quant_tokens(u))
            for unit in unit_at.get(t - 4, []):
                late.append(lambda u=unit: quant_rows(u))
            for b, it in fill_at.get(t, []):
                late.append(lambda b=b, it=it: fill_hi(b, it))
            for b, it in plan_at.get(t, []):
                late.append(lambda b=b, it=it: plan_product(b, it))
            for b, it in fill_at.get(t, []):
                late.append(lambda b=b, it=it: fill_lo(b, it))
            for b, it in plan_at.get(t, []):
                late.append(lambda b=b, it=it: plan_cost(b, it))
            if t in step_at:
                while len(mx) < WIDE:
                    mx.append(spare)
                for i in range(KICK):
                    mx.pop(0)()
                half_step(step_at[t][0], step_at[t][1], mx)
            else:
                for call in mx:
                    call()
            for call in turns + late:
                call()

        tp = psum.tile([P, TAIL_COL + 1], F32, name="tp", tag="mm", bufs=8)
        nc.tensor.matmul(out=tp[:], lhsT=ones_f[:], rhs=ota[:], start=True, stop=True)
        tot = small.tile([P, 1], F32, name="tot", tag="tot")
        nc.vector.tensor_reduce(out=tot[:], in_=tp[:], axis=AX.X, op=ALU.add)
        res = small.tile([P, 1], F32, name="res", tag="res")
        nc.vector.tensor_scalar_mul(out=res[:], in0=tot[:], scalar1=-1.0 / B)
        o1 = out_1
        if o1.ndim == 0:
            o1 = o1.unsqueeze(0)
        if o1.ndim == 1:
            o1 = o1.unsqueeze(0)
        nc.sync.dma_start(out=o1, in_=res[0:1, 0:1])
